import numpy as np
import ml_dtypes


def mxq(x, axis, fmt="e4m3"):
    dtype, down = {"e4m3": (ml_dtypes.float8_e4m3fn, 7), "e5m2": (ml_dtypes.float8_e5m2, 14)}[fmt]
    v = np.moveaxis(np.asarray(x, np.float32).astype(ml_dtypes.bfloat16).astype(np.float64), axis, -1)
    blocks = v.reshape(v.shape[:-1] + (-1, 32))
    amax = np.abs(blocks).max(-1, keepdims=True)
    byte = np.maximum(np.where(amax > 0, np.frexp(amax)[1] - 1 + 127, 0) - down, 1)
    scale = np.exp2(byte - 127.0)
    codes = (blocks / scale).astype(np.float32).astype(dtype).astype(np.float64)
    return np.moveaxis((codes * scale).reshape(v.shape), -1, axis)


WIDE = False


def mx_kscale(k):
    if not WIDE:
        return np.ones(k)
    levels = np.array([10, -10, 5, -5, 0])
    a = np.random.permutation(np.resize(levels, k // 512 * 4)).reshape(k // 512, 4)
    idx = np.arange(k)
    return np.exp2(a[idx // 512, idx % 128 // 32])


BF16 = ml_dtypes.bfloat16


def bf(x):
    return np.asarray(x, np.float32).astype(BF16)


def f64(x):
    return np.asarray(x).astype(np.float64)


B, H, S, D, BS = 2, 12, 1024, 128, 512
NB = S // BS
NEG_INF = -10000.0


def setup_inputs():
    c = np.sqrt(2.0) / D ** 0.25
    s = np.tile(mx_kscale(BS), NB)
    Q = np.random.standard_normal((B, H, S, D)) * c
    K = np.random.standard_normal((B, H, S, D)) * c
    V = np.random.standard_normal((B, H, S, D))
    Q[..., 0] = 1.0
    K[..., 0] += np.log(s)
    V = V / s[:, None] * s.mean()
    return {"Q": bf(Q), "K": bf(K), "V": bf(V),
            "mask": bf((np.random.random((B, S)) < 0.8).astype(np.float64))}


def reference(Q, K, V, mask):
    Qb = f64(Q).reshape(B, H, NB, BS, D)
    Kb = f64(K).reshape(B, H, NB, BS, D)
    Vb = f64(V).reshape(B, H, NB, BS, D)
    m = f64(mask)
    scores = Qb @ Kb.transpose(0, 1, 2, 4, 3)
    remove = (m == 0.0).reshape(B, 1, NB, 1, BS)
    scores = scores + np.where(remove, NEG_INF, 0.0)
    e = np.exp(scores - scores.max(-1, keepdims=True))
    q_removed = (m == 0.0).reshape(B, 1, NB, BS, 1)
    ez = np.where(q_removed, 0.0, e)
    out = (mxq(ez, 4, "e4m3") @ mxq(Vb, 3, "e4m3")) / e.sum(-1, keepdims=True)
    return out.reshape(B, H, S, D)

@@ -1,0 +1,188 @@
+from contextlib import ExitStack
+
+import concourse.mybir as mybir
+from concourse.masks import make_identity
+
+BF16 = mybir.dt.bfloat16
+F32 = mybir.dt.float32
+U32 = mybir.dt.uint32
+U8 = mybir.dt.uint8
+FP8X4 = mybir.dt.float8_e4m3fn_x4
+ALU = mybir.AluOpType
+ACT = mybir.ActivationFunctionType
+AX = mybir.AxisListType
+
+P = 128
+B, H, S, D, BS = 2, 12, 1024, 128, 512
+NB = S // BS
+UNITS = B * H * NB
+T = BS // P
+GROUP = 4
+NEG = -10000.0
+FLOPS = 2 * 2 * BS * BS * D * UNITS
+
+
+def tile_localselfattention_kernel(tc, Q, K, V, mask, out):
+    nc = tc.nc
+    qf = Q.flatten_outer_dims()
+    kf = K.flatten_outer_dims()
+    vf = V.flatten_outer_dims()
+    of = out.flatten_outer_dims()
+
+    with ExitStack() as ctx:
+        const = ctx.enter_context(tc.tile_pool(name="const", bufs=1))
+        loads = ctx.enter_context(tc.tile_pool(name="loads", bufs=3))
+        vpool = ctx.enter_context(tc.tile_pool(name="vpool", bufs=2))
+        work = ctx.enter_context(tc.tile_pool(name="work", bufs=3))
+        stat = ctx.enter_context(tc.tile_pool(name="stat", bufs=8))
+        ps_t = ctx.enter_context(tc.psum_pool(name="ps_t", bufs=1))
+        ps_s = ctx.enter_context(tc.psum_pool(name="ps_s", bufs=3))
+        ps_e = ctx.enter_context(tc.psum_pool(name="ps_e", bufs=2))
+        ps_o = ctx.enter_context(tc.psum_pool(name="ps_o", bufs=2))
+
+        ident_bf = const.tile([P, P], BF16, name="ident_bf")
+        make_identity(nc, ident_bf[:])
+        ident_f = const.tile([P, P], F32, name="ident_f")
+        make_identity(nc, ident_f[:])
+
+        mk = const.tile([P, B, NB, T], BF16, name="mk")
+        with nc.allow_non_contiguous_dma(reason="the mask, four positions to a partition"):
+            nc.sync.dma_start(out=mk[:], in_=mask.rearrange("b (n p t) -> p b n t", p=P, t=T))
+        mkf = mk[:].rearrange("p b n t -> p (b n t)")
+        keepq = const.tile([P, B * NB * T], F32, name="keepq")
+        nc.vector.tensor_single_scalar(out=keepq[:], in_=mkf, scalar=0.0, op=ALU.not_equal)
+        bcol = const.tile([P, B * NB * T], F32, name="bcol")
+        nc.vector.tensor_scalar(
+            out=bcol[:], in0=mkf, scalar1=0.0, scalar2=NEG, op0=ALU.is_equal, op1=ALU.mult
+        )
+        bt = const.tile([P, B * NB * T, P], F32, name="bt")
+        nc.vector.tensor_copy(out=bt[:], in_=bcol[:].unsqueeze(2).to_broadcast([P, B * NB * T, P]))
+
+        raw = {}
+        vq = {}
+
+        def load_group(g):
+            rows = slice(g * GROUP * BS, (g + 1) * GROUP * BS)
+            tiles = []
+            for src, tag in ((qf, "q_raw"), (kf, "k_raw"), (vf, "v_raw")):
+                t_raw = loads.tile([P, GROUP, T, D], BF16, name=tag, tag=tag)
+                nc.sync.dma_start(
+                    out=t_raw[:], in_=src[rows, :].rearrange("(u p t) d -> p u t d", p=P, t=T)
+                )
+                tiles.append(t_raw)
+            raw[g] = tiles
+
+        def quantise_v(g):
+            v_raw = raw[g][2]
+            vg = vpool.tile([P, GROUP, D, T], BF16, name="vg", tag="vg", align_bytes=64)
+            nc.vector.tensor_copy(out=vg[:], in_=v_raw[:].rearrange("p u j d -> p u d j"))
+            vcodes = vpool.tile([P, GROUP * D], U32, name="vcodes", tag="vcodes", align_bytes=64)
+            vscales = vpool.tile([P, GROUP * D], U8, name="vscales", tag="vscales", align_bytes=64)
+            nc.vector.quantize_mx(
+                out=vcodes[:].bitcast(FP8X4),
+                scales=vscales[:],
+                in_=vg[:].rearrange("p u d j -> p (u d j)"),
+            )
+            vq[g] = (vcodes, vscales)
+
+        def unit(u):
+            g, ul = divmod(u, GROUP)
+            b = u // (H * NB)
+            n = u % NB
+            mg = b * NB + n
+            q_raw, k_raw = raw[g][0], raw[g][1]
+
+            qkT_ps = ps_t.tile([P, 2 * T, P], BF16, name="qkT_ps", tag="qkT_ps")
+            for t in range(T):
+                nc.tensor.transpose(qkT_ps[:, t, :], q_raw[:, ul, t, :], ident_bf[:])
+            for t in range(T):
+                nc.tensor.transpose(qkT_ps[:, T + t, :], k_raw[:, ul, t, :], ident_bf[:])
+            qkT = work.tile([P, 2 * T, P], BF16, name="qkT", tag="qkT")
+            nc.vector.tensor_copy(out=qkT[:], in_=qkT_ps[:])
+
+            e_sb = work.tile([P, T, BS], BF16, name="e_sb", tag="e_sb")
+            eg = work.tile([P, T, P, T], BF16, name="eg", tag="eg", align_bytes=64)
+            rsum = stat.tile([P, T], F32, name="rsum", tag="rsum")
+            for i in range(T):
+                s_ps = ps_s.tile([P, BS], F32, name="s_ps", tag="s_ps")
+                for t in range(T):
+                    nc.tensor.matmul(
+                        out=s_ps[:, t * P : (t + 1) * P],
+                        lhsT=bt[:, mg * T + t, :],
+                        rhs=ident_f[:],
+                        is_transpose=True,
+                        start=(t == 0),
+                        stop=False,
+                    )
+                nc.tensor.matmul(
+                    out=s_ps[:],
+                    lhsT=qkT[:, i, :],
+                    rhs=qkT[:, T : 2 * T, :].rearrange("p t k -> p (t k)"),
+                    start=False,
+                    stop=True,
+                )
+                negm = stat.tile([P, 1], F32, name="negm", tag="negm")
+                nc.vector.tensor_reduce(out=negm[:], in_=s_ps[:], axis=AX.X, op=ALU.max, negate=True)
+                nc.scalar.activation(
+                    out=e_sb[:, i, :],
+                    in_=s_ps[:],
+                    func=ACT.Exp,
+                    bias=negm[:],
+                    scale=1.0,
+                    accum_out=rsum[:, i : i + 1],
+                )
+                if i % 2 == 1:
+                    eT_ps = ps_e.tile([P, 2, T, P], BF16, name="eT_ps", tag="eT_ps")
+                    for ii in range(2):
+                        for j in range(T):
+                            nc.tensor.transpose(
+                                eT_ps[:, ii, j, :],
+                                e_sb[:, i - 1 + ii, j * P : (j + 1) * P],
+                                ident_bf[:],
+                            )
+                    nc.scalar.copy(
+                        out=eg[:, i - 1 : i + 1, :, :],
+                        in_=eT_ps[:].rearrange("p i j q -> p i q j"),
+                    )
+
+            ecodes = work.tile([P, BS], U32, name="ecodes", tag="ecodes", align_bytes=64)
+            escales = work.tile([P, BS], U8, name="escales", tag="escales", align_bytes=64)
+            nc.vector.quantize_mx(
+                out=ecodes[:].bitcast(FP8X4),
+                scales=escales[:],
+                in_=eg[:].rearrange("p i q j -> p (i q j)"),
+            )
+            rinv = stat.tile([P, T], F32, name="rinv", tag="rinv")
+            nc.vector.reciprocal(out=rinv[:], in_=rsum[:])
+            rk = stat.tile([P, T], F32, name="rk", tag="rk")
+            nc.vector.tensor_tensor(
+                out=rk[:], in0=rinv[:], in1=keepq[:, mg * T : (mg + 1) * T], op=ALU.mult
+            )
+            vcodes, vscales = vq[g]
+            pv_ps = ps_o.tile([P, T, D], F32, name="pv_ps", tag="pv_ps")
+            for i in range(T):
+                nc.tensor.matmul_mx(
+                    out=pv_ps[:, i, :],
+                    lhsT=ecodes[:, i * P : (i + 1) * P].bitcast(FP8X4),
+                    lhsT_scale=escales[:, i * P : (i + 1) * P],
+                    rhs=vcodes[:, ul * D : (ul + 1) * D].bitcast(FP8X4),
+                    rhs_scale=vscales[:, ul * D : (ul + 1) * D],
+                    start=True,
+                    stop=True,
+                )
+            o_sb = work.tile([P, T, D], F32, name="o_sb", tag="o_sb")
+            nc.vector.tensor_tensor(
+                out=o_sb[:],
+                in0=pv_ps[:],
+                in1=rk[:].unsqueeze(2).to_broadcast([P, T, D]),
+                op=ALU.mult,
+            )
+            nc.gpsimd.dma_start(
+                out=of[u * BS : (u + 1) * BS, :].rearrange("(p t) d -> p t d", t=T), in_=o_sb[:]
+            )
+
+        for u in range(UNITS):
+            if u % GROUP == 0:
+                load_group(u // GROUP)
+                quantise_v(u // GROUP)
+            unit(u)

@@ -17,7 +17,9 @@ B, H, S, D, BS = 2, 12, 1024, 128, 512
 NB = S // BS
 UNITS = B * H * NB
 T = BS // P
-GROUP = 4
+GROUP = 2
+NGROUPS = UNITS // GROUP
+LOAD_BUFS = 4
 NEG = -10000.0
 FLOPS = 2 * 2 * BS * BS * D * UNITS
 
@@ -30,38 +32,23 @@ def tile_localselfattention_kernel(tc, Q, K, V, mask, out):
     of = out.flatten_outer_dims()
 
     with ExitStack() as ctx:
+        ctx.enter_context(tc.manual_schedule())
         const = ctx.enter_context(tc.tile_pool(name="const", bufs=1))
-        loads = ctx.enter_context(tc.tile_pool(name="loads", bufs=3))
-        vpool = ctx.enter_context(tc.tile_pool(name="vpool", bufs=2))
+        loads = ctx.enter_context(tc.tile_pool(name="loads", bufs=LOAD_BUFS))
+        vpool = ctx.enter_context(tc.tile_pool(name="vpool", bufs=4))
         work = ctx.enter_context(tc.tile_pool(name="work", bufs=3))
         stat = ctx.enter_context(tc.tile_pool(name="stat", bufs=8))
         ps_t = ctx.enter_context(tc.psum_pool(name="ps_t", bufs=1))
-        ps_s = ctx.enter_context(tc.psum_pool(name="ps_s", bufs=3))
+        ps_s = ctx.enter_context(tc.psum_pool(name="ps_s", bufs=4))
         ps_e = ctx.enter_context(tc.psum_pool(name="ps_e", bufs=2))
-        ps_o = ctx.enter_context(tc.psum_pool(name="ps_o", bufs=2))
-
-        ident_bf = const.tile([P, P], BF16, name="ident_bf")
-        make_identity(nc, ident_bf[:])
-        ident_f = const.tile([P, P], F32, name="ident_f")
-        make_identity(nc, ident_f[:])
-
-        mk = const.tile([P, B, NB, T], BF16, name="mk")
-        with nc.allow_non_contiguous_dma(reason="the mask, four positions to a partition"):
-            nc.sync.dma_start(out=mk[:], in_=mask.rearrange("b (n p t) -> p b n t", p=P, t=T))
-        mkf = mk[:].rearrange("p b n t -> p (b n t)")
-        keepq = const.tile([P, B * NB * T], F32, name="keepq")
-        nc.vector.tensor_single_scalar(out=keepq[:], in_=mkf, scalar=0.0, op=ALU.not_equal)
-        bcol = const.tile([P, B * NB * T], F32, name="bcol")
-        nc.vector.tensor_scalar(
-            out=bcol[:], in0=mkf, scalar1=0.0, scalar2=NEG, op0=ALU.is_equal, op1=ALU.mult
-        )
-        bt = const.tile([P, B * NB * T, P], F32, name="bt")
-        nc.vector.tensor_copy(out=bt[:], in_=bcol[:].unsqueeze(2).to_broadcast([P, B * NB * T, P]))
+        ps_o = ctx.enter_context(tc.psum_pool(name="ps_o", bufs=1))
 
         raw = {}
-        vq = {}
+        st = {}
 
         def load_group(g):
+            if g >= NGROUPS:
+                return
             rows = slice(g * GROUP * BS, (g + 1) * GROUP * BS)
             tiles = []
             for src, tag in ((qf, "q_raw"), (kf, "k_raw"), (vf, "v_raw")):
@@ -72,108 +59,160 @@ def tile_localselfattention_kernel(tc, Q, K, V, mask, out):
                 tiles.append(t_raw)
             raw[g] = tiles
 
-        def quantise_v(g):
-            v_raw = raw[g][2]
-            vg = vpool.tile([P, GROUP, D, T], BF16, name="vg", tag="vg", align_bytes=64)
-            nc.vector.tensor_copy(out=vg[:], in_=v_raw[:].rearrange("p u j d -> p u d j"))
-            vcodes = vpool.tile([P, GROUP * D], U32, name="vcodes", tag="vcodes", align_bytes=64)
-            vscales = vpool.tile([P, GROUP * D], U8, name="vscales", tag="vscales", align_bytes=64)
-            nc.vector.quantize_mx(
-                out=vcodes[:].bitcast(FP8X4),
-                scales=vscales[:],
-                in_=vg[:].rearrange("p u d j -> p (u d j)"),
-            )
-            vq[g] = (vcodes, vscales)
+        mk = const.tile([P, B, NB, T], BF16, name="mk")
+        with nc.allow_non_contiguous_dma(reason="the mask, four positions to a partition"):
+            nc.sync.dma_start(out=mk[:], in_=mask.rearrange("b (n p t) -> p b n t", p=P, t=T))
+        for g in range(LOAD_BUFS):
+            load_group(g)
 
-        def unit(u):
+        ident_bf = const.tile([P, P], BF16, name="ident_bf")
+        make_identity(nc, ident_bf[:])
+        ident_f = const.tile([P, P], F32, name="ident_f")
+        make_identity(nc, ident_f[:])
+
+        mkf = mk[:].rearrange("p b n t -> p (b n t)")
+        keepq = const.tile([P, B * NB * T], F32, name="keepq")
+        nc.vector.tensor_single_scalar(out=keepq[:], in_=mkf, scalar=0.0, op=ALU.not_equal)
+        bcol = const.tile([P, B * NB * T], F32, name="bcol")
+        nc.vector.tensor_scalar(
+            out=bcol[:], in0=mkf, scalar1=0.0, scalar2=NEG, op0=ALU.is_equal, op1=ALU.mult
+        )
+        bt = const.tile([P, B * NB * T, P], F32, name="bt")
+        nc.vector.tensor_copy(out=bt[:], in_=bcol[:].unsqueeze(2).to_broadcast([P, B * NB * T, P]))
+
+        def ok(u):
+            return 0 <= u < UNITS
+
+        def mask_group(u):
+            return (u // (H * NB)) * NB + u % NB
+
+        def pe_qk_transposes(u):
+            if not ok(u):
+                return
             g, ul = divmod(u, GROUP)
-            b = u // (H * NB)
-            n = u % NB
-            mg = b * NB + n
-            q_raw, k_raw = raw[g][0], raw[g][1]
-
             qkT_ps = ps_t.tile([P, 2 * T, P], BF16, name="qkT_ps", tag="qkT_ps")
             for t in range(T):
-                nc.tensor.transpose(qkT_ps[:, t, :], q_raw[:, ul, t, :], ident_bf[:])
+                nc.tensor.transpose(qkT_ps[:, t, :], raw[g][0][:, ul, t, :], ident_bf[:])
             for t in range(T):
-                nc.tensor.transpose(qkT_ps[:, T + t, :], k_raw[:, ul, t, :], ident_bf[:])
-            qkT = work.tile([P, 2 * T, P], BF16, name="qkT", tag="qkT")
-            nc.vector.tensor_copy(out=qkT[:], in_=qkT_ps[:])
+                nc.tensor.transpose(qkT_ps[:, T + t, :], raw[g][1][:, ul, t, :], ident_bf[:])
+            st[("qkT_ps", u)] = qkT_ps
 
-            e_sb = work.tile([P, T, BS], BF16, name="e_sb", tag="e_sb")
-            eg = work.tile([P, T, P, T], BF16, name="eg", tag="eg", align_bytes=64)
-            rsum = stat.tile([P, T], F32, name="rsum", tag="rsum")
-            for i in range(T):
-                s_ps = ps_s.tile([P, BS], F32, name="s_ps", tag="s_ps")
-                for t in range(T):
-                    nc.tensor.matmul(
-                        out=s_ps[:, t * P : (t + 1) * P],
-                        lhsT=bt[:, mg * T + t, :],
-                        rhs=ident_f[:],
-                        is_transpose=True,
-                        start=(t == 0),
-                        stop=False,
-                    )
+        def pe_scores(u, i):
+            if not ok(u):
+                return
+            mg = mask_group(u)
+            qkT = st[("qkT", u)]
+            s_ps = ps_s.tile([P, BS], F32, name="s_ps", tag="s_ps")
+            for t in range(T):
                 nc.tensor.matmul(
-                    out=s_ps[:],
-                    lhsT=qkT[:, i, :],
-                    rhs=qkT[:, T : 2 * T, :].rearrange("p t k -> p (t k)"),
-                    start=False,
-                    stop=True,
+                    out=s_ps[:, t * P : (t + 1) * P],
+                    lhsT=bt[:, mg * T + t, :],
+                    rhs=ident_f[:],
+                    is_transpose=True,
+                    start=(t == 0),
+                    stop=False,
                 )
-                negm = stat.tile([P, 1], F32, name="negm", tag="negm")
-                nc.vector.tensor_reduce(out=negm[:], in_=s_ps[:], axis=AX.X, op=ALU.max, negate=True)
-                nc.scalar.activation(
-                    out=e_sb[:, i, :],
-                    in_=s_ps[:],
-                    func=ACT.Exp,
-                    bias=negm[:],
-                    scale=1.0,
-                    accum_out=rsum[:, i : i + 1],
-                )
-                if i % 2 == 1:
-                    eT_ps = ps_e.tile([P, 2, T, P], BF16, name="eT_ps", tag="eT_ps")
-                    for ii in range(2):
-                        for j in range(T):
-                            nc.tensor.transpose(
-                                eT_ps[:, ii, j, :],
-                                e_sb[:, i - 1 + ii, j * P : (j + 1) * P],
-                                ident_bf[:],
-                            )
-                    nc.scalar.copy(
-                        out=eg[:, i - 1 : i + 1, :, :],
-                        in_=eT_ps[:].rearrange("p i j q -> p i q j"),
-                    )
+            nc.tensor.matmul(
+                out=s_ps[:],
+                lhsT=qkT[:, i, :],
+                rhs=qkT[:, T : 2 * T, :].rearrange("p t k -> p (t k)"),
+                start=False,
+                stop=True,
+            )
+            st[("s_ps", u, i)] = s_ps
 
-            ecodes = work.tile([P, BS], U32, name="ecodes", tag="ecodes", align_bytes=64)
-            escales = work.tile([P, BS], U8, name="escales", tag="escales", align_bytes=64)
-            nc.vector.quantize_mx(
-                out=ecodes[:].bitcast(FP8X4),
-                scales=escales[:],
-                in_=eg[:].rearrange("p i q j -> p (i q j)"),
-            )
-            rinv = stat.tile([P, T], F32, name="rinv", tag="rinv")
-            nc.vector.reciprocal(out=rinv[:], in_=rsum[:])
-            rk = stat.tile([P, T], F32, name="rk", tag="rk")
-            nc.vector.tensor_tensor(
-                out=rk[:], in0=rinv[:], in1=keepq[:, mg * T : (mg + 1) * T], op=ALU.mult
-            )
-            vcodes, vscales = vq[g]
+        def pe_e_transposes(u, h):
+            if not ok(u):
+                return
+            e_sb = st[("e_sb", u, h)]
+            eT_ps = ps_e.tile([P, 2, T, P], BF16, name="eT_ps", tag="eT_ps")
+            for ii in range(2):
+                for j in range(T):
+                    nc.tensor.transpose(
+                        eT_ps[:, ii, j, :], e_sb[:, ii, j * P : (j + 1) * P], ident_bf[:]
+                    )
+            st[("eT_ps", u, h)] = eT_ps
+
+        def pe_pv(u):
+            if not ok(u):
+                return
+            ecodes, escales = st[("eq", u)]
+            vcodes, vscales = st[("vq", u)]
             pv_ps = ps_o.tile([P, T, D], F32, name="pv_ps", tag="pv_ps")
             for i in range(T):
                 nc.tensor.matmul_mx(
                     out=pv_ps[:, i, :],
                     lhsT=ecodes[:, i * P : (i + 1) * P].bitcast(FP8X4),
                     lhsT_scale=escales[:, i * P : (i + 1) * P],
-                    rhs=vcodes[:, ul * D : (ul + 1) * D].bitcast(FP8X4),
-                    rhs_scale=vscales[:, ul * D : (ul + 1) * D],
+                    rhs=vcodes[:].bitcast(FP8X4),
+                    rhs_scale=vscales[:],
                     start=True,
                     stop=True,
                 )
+            st[("pv_ps", u)] = pv_ps
+
+        def ve_qk_copy(u):
+            if not ok(u):
+                return
+            qkT = work.tile([P, 2 * T, P], BF16, name="qkT", tag="qkT")
+            nc.vector.tensor_copy(out=qkT[:], in_=st[("qkT_ps", u)][:])
+            st[("qkT", u)] = qkT
+
+        def ve_max(u, i):
+            if not ok(u):
+                return
+            negm = stat.tile([P, 1], F32, name="negm", tag="negm")
+            nc.vector.tensor_reduce(
+                out=negm[:], in_=st[("s_ps", u, i)][:], axis=AX.X, op=ALU.max, negate=True
+            )
+            st[("negm", u, i)] = negm
+
+        def ve_v_regroup(u):
+            if not ok(u):
+                return
+            g, ul = divmod(u, GROUP)
+            vg = vpool.tile([P, D, T], BF16, name="vg", tag="vg", align_bytes=64)
+            nc.vector.tensor_copy(out=vg[:], in_=raw[g][2][:, ul, :, :].rearrange("p j d -> p d j"))
+            st[("vg", u)] = vg
+
+        def ve_v_quantise(u):
+            if not ok(u):
+                return
+            vcodes = vpool.tile([P, D], U32, name="vcodes", tag="vcodes", align_bytes=64)
+            vscales = vpool.tile([P, D], U8, name="vscales", tag="vscales", align_bytes=64)
+            nc.vector.quantize_mx(
+                out=vcodes[:].bitcast(FP8X4),
+                scales=vscales[:],
+                in_=st[("vg", u)][:].rearrange("p d j -> p (d j)"),
+            )
+            st[("vq", u)] = (vcodes, vscales)
+
+        def ve_e_quantise(u):
+            if not ok(u):
+                return
+            ecodes = work.tile([P, BS], U32, name="ecodes", tag="ecodes", align_bytes=64)
+            escales = work.tile([P, BS], U8, name="escales", tag="escales", align_bytes=64)
+            nc.vector.quantize_mx(
+                out=ecodes[:].bitcast(FP8X4),
+                scales=escales[:],
+                in_=st[("eg", u)][:].rearrange("p i q j -> p (i q j)"),
+            )
+            st[("eq", u)] = (ecodes, escales)
+
+        def ve_out(u):
+            if not ok(u):
+                return
+            mg = mask_group(u)
+            rinv = stat.tile([P, T], F32, name="rinv", tag="rinv")
+            nc.vector.reciprocal(out=rinv[:], in_=st[("rsum", u)][:])
+            rk = stat.tile([P, T], F32, name="rk", tag="rk")
+            nc.vector.tensor_tensor(
+                out=rk[:], in0=rinv[:], in1=keepq[:, mg * T : (mg + 1) * T], op=ALU.mult
+            )
             o_sb = work.tile([P, T, D], F32, name="o_sb", tag="o_sb")
             nc.vector.tensor_tensor(
                 out=o_sb[:],
-                in0=pv_ps[:],
+                in0=st[("pv_ps", u)][:],
                 in1=rk[:].unsqueeze(2).to_broadcast([P, T, D]),
                 op=ALU.mult,
             )
@@ -181,8 +220,63 @@ def tile_localselfattention_kernel(tc, Q, K, V, mask, out):
                 out=of[u * BS : (u + 1) * BS, :].rearrange("(p t) d -> p t d", t=T), in_=o_sb[:]
             )
 
-        for u in range(UNITS):
-            if u % GROUP == 0:
-                load_group(u // GROUP)
-                quantise_v(u // GROUP)
-            unit(u)
+        def se_exp(u, i):
+            if not ok(u):
+                return
+            h, ii = divmod(i, 2)
+            if i == 0:
+                st[("rsum", u)] = stat.tile([P, T], F32, name="rsum", tag="rsum")
+            if ii == 0:
+                st[("e_sb", u, h)] = work.tile([P, 2, BS], BF16, name="e_sb", tag="e_sb")
+            nc.scalar.activation(
+                out=st[("e_sb", u, h)][:, ii, :],
+                in_=st[("s_ps", u, i)][:],
+                func=ACT.Exp,
+                bias=st[("negm", u, i)][:],
+                scale=1.0,
+                accum_out=st[("rsum", u)][:, i : i + 1],
+            )
+
+        def se_e_copy(u, h):
+            if not ok(u):
+                return
+            if h == 0:
+                st[("eg", u)] = work.tile([P, T, P, T], BF16, name="eg", tag="eg", align_bytes=64)
+            nc.scalar.copy(
+                out=st[("eg", u)][:, 2 * h : 2 * h + 2, :, :],
+                in_=st[("eT_ps", u, h)][:].rearrange("p i j q -> p i q j"),
+            )
+
+        pe_qk_transposes(0)
+        ve_qk_copy(0)
+        ve_v_regroup(0)
+        for s in range(4 * UNITS + 12):
+            u, i = divmod(s, 4)
+            if i == 3:
+                pe_qk_transposes(u + 1)
+            pe_scores(u, i)
+            if i == 0:
+                pe_e_transposes(u - 1, 0)
+            elif i == 1:
+                pe_pv(u - 2)
+            elif i == 2:
+                pe_e_transposes(u - 1, 1)
+            um, im = divmod(s - 1, 4)
+            ve_max(um, im)
+            if i == 0:
+                ve_e_quantise(u - 2)
+            elif i == 1:
+                ve_v_regroup(u + 1)
+                ve_v_quantise(u)
+            elif i == 2:
+                ve_out(u - 2)
+            else:
+                ve_qk_copy(u + 1)
+            ux, ix = divmod(s - 2, 4)
+            se_exp(ux, ix)
+            if i == 1:
+                se_e_copy(u - 1, 0)
+            elif i == 3:
+                se_e_copy(u - 1, 1)
+                if (u + 1) % GROUP == GROUP - 1:
+                    load_group((u + 1) // GROUP + LOAD_BUFS)

@@ -172,7 +172,14 @@ def tile_localselfattention_kernel(tc, Q, K, V, mask, out):
                 return
             g, ul = divmod(u, GROUP)
             vg = vpool.tile([P, D, T], BF16, name="vg", tag="vg", align_bytes=64)
-            nc.vector.tensor_copy(out=vg[:], in_=raw[g][2][:, ul, :, :].rearrange("p j d -> p d j"))
+            nc.gpsimd.tensor_scalar(
+                out=vg[:],
+                in0=raw[g][2][:, ul, :, :].rearrange("p j d -> p d j"),
+                scalar1=1.0,
+                scalar2=0.0,
+                op0=ALU.mult,
+                op1=ALU.add,
+            )
             st[("vg", u)] = vg
 
         def ve_v_quantise(u):
@@ -216,7 +223,7 @@ def tile_localselfattention_kernel(tc, Q, K, V, mask, out):
                 in1=rk[:].unsqueeze(2).to_broadcast([P, T, D]),
                 op=ALU.mult,
             )
-            nc.gpsimd.dma_start(
+            nc.sync.dma_start(
                 out=of[u * BS : (u + 1) * BS, :].rearrange("(p t) d -> p t d", t=T), in_=o_sb[:]
             )
 
@@ -247,36 +254,34 @@ def tile_localselfattention_kernel(tc, Q, K, V, mask, out):
                 in_=st[("eT_ps", u, h)][:].rearrange("p i j q -> p i q j"),
             )
 
-        pe_qk_transposes(0)
-        ve_qk_copy(0)
-        ve_v_regroup(0)
-        for s in range(4 * UNITS + 12):
+        for s in range(-4, 4 * UNITS + 13):
             u, i = divmod(s, 4)
-            if i == 3:
-                pe_qk_transposes(u + 1)
             pe_scores(u, i)
             if i == 0:
                 pe_e_transposes(u - 1, 0)
             elif i == 1:
-                pe_pv(u - 2)
+                pe_qk_transposes(u + 1)
             elif i == 2:
                 pe_e_transposes(u - 1, 1)
+            else:
+                pe_pv(u - 2)
+            if i == 0:
+                ve_v_regroup(u + 1)
             um, im = divmod(s - 1, 4)
             ve_max(um, im)
             if i == 0:
-                ve_e_quantise(u - 2)
+                ve_out(u - 3)
             elif i == 1:
-                ve_v_regroup(u + 1)
-                ve_v_quantise(u)
+                ve_e_quantise(u - 2)
             elif i == 2:
-                ve_out(u - 2)
-            else:
                 ve_qk_copy(u + 1)
+            else:
+                ve_v_quantise(u)
             ux, ix = divmod(s - 2, 4)
             se_exp(ux, ix)
             if i == 1:
                 se_e_copy(u - 1, 0)
-            elif i == 3:
-                se_e_copy(u - 1, 1)
                 if (u + 1) % GROUP == GROUP - 1:
                     load_group((u + 1) // GROUP + LOAD_BUFS)
+            elif i == 3:
+                se_e_copy(u - 1, 1)

@@ -38,6 +38,7 @@ def tile_localselfattention_kernel(tc, Q, K, V, mask, out):
         vpool = ctx.enter_context(tc.tile_pool(name="vpool", bufs=4))
         work = ctx.enter_context(tc.tile_pool(name="work", bufs=3))
         stat = ctx.enter_context(tc.tile_pool(name="stat", bufs=8))
+        spool = ctx.enter_context(tc.tile_pool(name="spool", bufs=5))
         ps_t = ctx.enter_context(tc.psum_pool(name="ps_t", bufs=1))
         ps_s = ctx.enter_context(tc.psum_pool(name="ps_s", bufs=4))
         ps_e = ctx.enter_context(tc.psum_pool(name="ps_e", bufs=2))
@@ -162,10 +163,18 @@ def tile_localselfattention_kernel(tc, Q, K, V, mask, out):
             if not ok(u):
                 return
             negm = stat.tile([P, 1], F32, name="negm", tag="negm")
-            nc.vector.tensor_reduce(
-                out=negm[:], in_=st[("s_ps", u, i)][:], axis=AX.X, op=ALU.max, negate=True
+            sneg = spool.tile([P, BS], F32, name="sneg", tag="sneg")
+            nc.vector.tensor_scalar(
+                out=sneg[:],
+                in0=st[("s_ps", u, i)][:],
+                scalar1=-1.0,
+                scalar2=None,
+                op0=ALU.mult,
+                op1=ALU.min,
+                accum_out=negm[:],
             )
             st[("negm", u, i)] = negm
+            st[("sneg", u, i)] = sneg
 
         def ve_v_regroup(u):
             if not ok(u):
@@ -237,10 +246,10 @@ def tile_localselfattention_kernel(tc, Q, K, V, mask, out):
                 st[("e_sb", u, h)] = work.tile([P, 2, BS], BF16, name="e_sb", tag="e_sb")
             nc.scalar.activation(
                 out=st[("e_sb", u, h)][:, ii, :],
-                in_=st[("s_ps", u, i)][:],
+                in_=st[("sneg", u, i)][:],
                 func=ACT.Exp,
                 bias=st[("negm", u, i)][:],
-                scale=1.0,
+                scale=-1.0,
                 accum_out=st[("rsum", u)][:, i : i + 1],
             )
 

@@ -18,6 +18,7 @@ NB = S // BS
 UNITS = B * H * NB
 T = BS // P
 GROUP = 2
+VBATCH = 4
 NGROUPS = UNITS // GROUP
 LOAD_BUFS = 4
 NEG = -10000.0
@@ -30,15 +31,15 @@ def tile_localselfattention_kernel(tc, Q, K, V, mask, out):
     kf = K.flatten_outer_dims()
     vf = V.flatten_outer_dims()
     of = out.flatten_outer_dims()
+    NM = B * NB * T
 
     with ExitStack() as ctx:
         ctx.enter_context(tc.manual_schedule())
         const = ctx.enter_context(tc.tile_pool(name="const", bufs=1))
         loads = ctx.enter_context(tc.tile_pool(name="loads", bufs=LOAD_BUFS))
-        vpool = ctx.enter_context(tc.tile_pool(name="vpool", bufs=4))
+        vpool = ctx.enter_context(tc.tile_pool(name="vpool", bufs=3))
         work = ctx.enter_context(tc.tile_pool(name="work", bufs=3))
         stat = ctx.enter_context(tc.tile_pool(name="stat", bufs=8))
-        spool = ctx.enter_context(tc.tile_pool(name="spool", bufs=5))
         ps_t = ctx.enter_context(tc.psum_pool(name="ps_t", bufs=1))
         ps_s = ctx.enter_context(tc.psum_pool(name="ps_s", bufs=4))
         ps_e = ctx.enter_context(tc.psum_pool(name="ps_e", bufs=2))
@@ -72,14 +73,21 @@ def tile_localselfattention_kernel(tc, Q, K, V, mask, out):
         make_identity(nc, ident_f[:])
 
         mkf = mk[:].rearrange("p b n t -> p (b n t)")
-        keepq = const.tile([P, B * NB * T], F32, name="keepq")
-        nc.vector.tensor_single_scalar(out=keepq[:], in_=mkf, scalar=0.0, op=ALU.not_equal)
-        bcol = const.tile([P, B * NB * T], F32, name="bcol")
+        bcol = const.tile([P, NM], F32, name="bcol")
         nc.vector.tensor_scalar(
             out=bcol[:], in0=mkf, scalar1=0.0, scalar2=NEG, op0=ALU.is_equal, op1=ALU.mult
         )
-        bt = const.tile([P, B * NB * T, P], F32, name="bt")
-        nc.vector.tensor_copy(out=bt[:], in_=bcol[:].unsqueeze(2).to_broadcast([P, B * NB * T, P]))
+        bt = const.tile([P, NM, P], F32, name="bt")
+        nc.vector.tensor_copy(out=bt[:], in_=bcol[:].unsqueeze(2).to_broadcast([P, NM, P]))
+        keepq = const.tile([P, NM], BF16, name="keepq")
+        nc.vector.tensor_single_scalar(out=keepq[:], in_=mkf, scalar=0.0, op=ALU.not_equal)
+        dq = const.tile([P, NM, P], BF16, name="dq")
+        nc.vector.tensor_tensor(
+            out=dq[:],
+            in0=ident_bf[:].unsqueeze(1).to_broadcast([P, NM, P]),
+            in1=keepq[:].unsqueeze(2).to_broadcast([P, NM, P]),
+            op=ALU.mult,
+        )
 
         def ok(u):
             return 0 <= u < UNITS
@@ -125,12 +133,15 @@ def tile_localselfattention_kernel(tc, Q, K, V, mask, out):
         def pe_e_transposes(u, h):
             if not ok(u):
                 return
+            mg = mask_group(u)
             e_sb = st[("e_sb", u, h)]
             eT_ps = ps_e.tile([P, 2, T, P], BF16, name="eT_ps", tag="eT_ps")
             for ii in range(2):
                 for j in range(T):
                     nc.tensor.transpose(
-                        eT_ps[:, ii, j, :], e_sb[:, ii, j * P : (j + 1) * P], ident_bf[:]
+                        eT_ps[:, ii, j, :],
+                        e_sb[:, ii, j * P : (j + 1) * P],
+                        dq[:, mg * T + 2 * h + ii, :],
                     )
             st[("eT_ps", u, h)] = eT_ps
 
@@ -138,70 +149,74 @@ def tile_localselfattention_kernel(tc, Q, K, V, mask, out):
             if not ok(u):
                 return
             ecodes, escales = st[("eq", u)]
-            vcodes, vscales = st[("vq", u)]
+            vcodes, vscales = st[("vq", u // VBATCH)]
+            cols = slice((u % VBATCH) * D, (u % VBATCH + 1) * D)
             pv_ps = ps_o.tile([P, T, D], F32, name="pv_ps", tag="pv_ps")
             for i in range(T):
                 nc.tensor.matmul_mx(
                     out=pv_ps[:, i, :],
                     lhsT=ecodes[:, i * P : (i + 1) * P].bitcast(FP8X4),
                     lhsT_scale=escales[:, i * P : (i + 1) * P],
-                    rhs=vcodes[:].bitcast(FP8X4),
-                    rhs_scale=vscales[:],
+                    rhs=vcodes[:, cols].bitcast(FP8X4),
+                    rhs_scale=vscales[:, cols],
                     start=True,
                     stop=True,
                 )
             st[("pv_ps", u)] = pv_ps
 
-        def ve_qk_copy(u):
-            if not ok(u):
-                return
-            qkT = work.tile([P, 2 * T, P], BF16, name="qkT", tag="qkT")
-            nc.vector.tensor_copy(out=qkT[:], in_=st[("qkT_ps", u)][:])
-            st[("qkT", u)] = qkT
-
-        def ve_max(u, i):
-            if not ok(u):
-                return
-            negm = stat.tile([P, 1], F32, name="negm", tag="negm")
-            sneg = spool.tile([P, BS], F32, name="sneg", tag="sneg")
-            nc.vector.tensor_scalar(
-                out=sneg[:],
-                in0=st[("s_ps", u, i)][:],
-                scalar1=-1.0,
-                scalar2=None,
-                op0=ALU.mult,
-                op1=ALU.min,
-                accum_out=negm[:],
-            )
-            st[("negm", u, i)] = negm
-            st[("sneg", u, i)] = sneg
-
-        def ve_v_regroup(u):
+        def gp_v_regroup(u):
             if not ok(u):
                 return
             g, ul = divmod(u, GROUP)
-            vg = vpool.tile([P, D, T], BF16, name="vg", tag="vg", align_bytes=64)
+            vb, vl = divmod(u, VBATCH)
+            if vl == 0:
+                st[("vg", vb)] = vpool.tile(
+                    [P, VBATCH, D, T], BF16, name="vg", tag="vg", align_bytes=64
+                )
             nc.gpsimd.tensor_scalar(
-                out=vg[:],
+                out=st[("vg", vb)][:, vl, :, :],
                 in0=raw[g][2][:, ul, :, :].rearrange("p j d -> p d j"),
                 scalar1=1.0,
                 scalar2=0.0,
                 op0=ALU.mult,
                 op1=ALU.add,
             )
-            st[("vg", u)] = vg
 
-        def ve_v_quantise(u):
+        def gp_e_regroup(u, i):
             if not ok(u):
                 return
-            vcodes = vpool.tile([P, D], U32, name="vcodes", tag="vcodes", align_bytes=64)
-            vscales = vpool.tile([P, D], U8, name="vscales", tag="vscales", align_bytes=64)
+            h, ii = divmod(i, 2)
+            if i == 0:
+                st[("eg", u)] = work.tile([P, T, P, T], BF16, name="eg", tag="eg", align_bytes=64)
+            nc.gpsimd.tensor_scalar(
+                out=st[("eg", u)][:, i, :, :],
+                in0=st[("ep", u, h)][:, ii, :, :].rearrange("p j q -> p q j"),
+                scalar1=1.0,
+                scalar2=0.0,
+                op0=ALU.mult,
+                op1=ALU.add,
+            )
+
+        def ve_max(u, i):
+            if not ok(u):
+                return
+            negm = stat.tile([P, 1], F32, name="negm", tag="negm")
+            nc.vector.tensor_reduce(
+                out=negm[:], in_=st[("s_ps", u, i)][:], axis=AX.X, op=ALU.max, negate=True
+            )
+            st[("negm", u, i)] = negm
+
+        def ve_v_quantise(vb):
+            if not 0 <= vb < UNITS // VBATCH:
+                return
+            vcodes = vpool.tile([P, VBATCH * D], U32, name="vcodes", tag="vcodes", align_bytes=64)
+            vscales = vpool.tile([P, VBATCH * D], U8, name="vscales", tag="vscales", align_bytes=64)
             nc.vector.quantize_mx(
                 out=vcodes[:].bitcast(FP8X4),
                 scales=vscales[:],
-                in_=st[("vg", u)][:].rearrange("p d j -> p (d j)"),
+                in_=st[("vg", vb)][:].rearrange("p u d j -> p (u d j)"),
             )
-            st[("vq", u)] = (vcodes, vscales)
+            st[("vq", vb)] = (vcodes, vscales)
 
         def ve_e_quantise(u):
             if not ok(u):
@@ -218,23 +233,25 @@ def tile_localselfattention_kernel(tc, Q, K, V, mask, out):
         def ve_out(u):
             if not ok(u):
                 return
-            mg = mask_group(u)
             rinv = stat.tile([P, T], F32, name="rinv", tag="rinv")
             nc.vector.reciprocal(out=rinv[:], in_=st[("rsum", u)][:])
-            rk = stat.tile([P, T], F32, name="rk", tag="rk")
-            nc.vector.tensor_tensor(
-                out=rk[:], in0=rinv[:], in1=keepq[:, mg * T : (mg + 1) * T], op=ALU.mult
-            )
             o_sb = work.tile([P, T, D], F32, name="o_sb", tag="o_sb")
             nc.vector.tensor_tensor(
                 out=o_sb[:],
                 in0=st[("pv_ps", u)][:],
-                in1=rk[:].unsqueeze(2).to_broadcast([P, T, D]),
+                in1=rinv[:].unsqueeze(2).to_broadcast([P, T, D]),
                 op=ALU.mult,
             )
             nc.sync.dma_start(
                 out=of[u * BS : (u + 1) * BS, :].rearrange("(p t) d -> p t d", t=T), in_=o_sb[:]
             )
+
+        def se_qk_copy(u):
+            if not ok(u):
+                return
+            qkT = work.tile([P, 2 * T, P], BF16, name="qkT", tag="qkT")
+            nc.scalar.copy(out=qkT[:], in_=st[("qkT_ps", u)][:])
+            st[("qkT", u)] = qkT
 
         def se_exp(u, i):
             if not ok(u):
@@ -246,51 +263,56 @@ def tile_localselfattention_kernel(tc, Q, K, V, mask, out):
                 st[("e_sb", u, h)] = work.tile([P, 2, BS], BF16, name="e_sb", tag="e_sb")
             nc.scalar.activation(
                 out=st[("e_sb", u, h)][:, ii, :],
-                in_=st[("sneg", u, i)][:],
+                in_=st[("s_ps", u, i)][:],
                 func=ACT.Exp,
                 bias=st[("negm", u, i)][:],
-                scale=-1.0,
+                scale=1.0,
                 accum_out=st[("rsum", u)][:, i : i + 1],
             )
 
         def se_e_copy(u, h):
             if not ok(u):
                 return
-            if h == 0:
-                st[("eg", u)] = work.tile([P, T, P, T], BF16, name="eg", tag="eg", align_bytes=64)
-            nc.scalar.copy(
-                out=st[("eg", u)][:, 2 * h : 2 * h + 2, :, :],
-                in_=st[("eT_ps", u, h)][:].rearrange("p i j q -> p i q j"),
-            )
+            ep = work.tile([P, 2, T, P], BF16, name="ep", tag="ep")
+            nc.scalar.copy(out=ep[:], in_=st[("eT_ps", u, h)][:])
+            st[("ep", u, h)] = ep
 
-        for s in range(-4, 4 * UNITS + 13):
+        for s in range(-20, 4 * UNITS + 16):
             u, i = divmod(s, 4)
             pe_scores(u, i)
             if i == 0:
                 pe_e_transposes(u - 1, 0)
             elif i == 1:
-                pe_qk_transposes(u + 1)
+                pe_pv(u - 3)
             elif i == 2:
                 pe_e_transposes(u - 1, 1)
             else:
-                pe_pv(u - 2)
+                pe_qk_transposes(u + 2)
+                if ok(u + 2) and (u + 2) % GROUP == GROUP - 1:
+                    load_group((u + 2) // GROUP + LOAD_BUFS)
             if i == 0:
-                ve_v_regroup(u + 1)
+                gp_e_regroup(u - 2, 2)
+            elif i == 1:
+                gp_e_regroup(u - 2, 3)
+                gp_v_regroup(u + 5)
+            elif i == 2:
+                gp_e_regroup(u - 1, 0)
+            else:
+                gp_e_regroup(u - 1, 1)
             um, im = divmod(s - 1, 4)
             ve_max(um, im)
             if i == 0:
-                ve_out(u - 3)
-            elif i == 1:
-                ve_e_quantise(u - 2)
+                if (u + 1) % VBATCH == 0:
+                    ve_v_quantise((u + 1) // VBATCH)
             elif i == 2:
-                ve_qk_copy(u + 1)
-            else:
-                ve_v_quantise(u)
+                ve_out(u - 3)
+            elif i == 3:
+                ve_e_quantise(u - 2)
             ux, ix = divmod(s - 2, 4)
             se_exp(ux, ix)
-            if i == 1:
+            if i == 0:
+                se_qk_copy(u + 1)
+            elif i == 1:
                 se_e_copy(u - 1, 0)
-                if (u + 1) % GROUP == GROUP - 1:
-                    load_group((u + 1) // GROUP + LOAD_BUFS)
             elif i == 3:
                 se_e_copy(u - 1, 1)

@@ -164,33 +164,31 @@ def tile_localselfattention_kernel(tc, Q, K, V, mask, out):
                 )
             st[("pv_ps", u)] = pv_ps
 
-        def gp_v_regroup(u):
-            if not ok(u):
+        def gp_v_regroup(g):
+            if not 0 <= g < NGROUPS:
                 return
-            g, ul = divmod(u, GROUP)
-            vb, vl = divmod(u, VBATCH)
+            vb, vl = divmod(g * GROUP, VBATCH)
             if vl == 0:
                 st[("vg", vb)] = vpool.tile(
                     [P, VBATCH, D, T], BF16, name="vg", tag="vg", align_bytes=64
                 )
             nc.gpsimd.tensor_scalar(
-                out=st[("vg", vb)][:, vl, :, :],
-                in0=raw[g][2][:, ul, :, :].rearrange("p j d -> p d j"),
+                out=st[("vg", vb)][:, vl : vl + GROUP, :, :],
+                in0=raw[g][2][:].rearrange("p u j d -> p u d j"),
                 scalar1=1.0,
                 scalar2=0.0,
                 op0=ALU.mult,
                 op1=ALU.add,
             )
 
-        def gp_e_regroup(u, i):
+        def gp_e_regroup(u, h):
             if not ok(u):
                 return
-            h, ii = divmod(i, 2)
-            if i == 0:
+            if h == 0:
                 st[("eg", u)] = work.tile([P, T, P, T], BF16, name="eg", tag="eg", align_bytes=64)
             nc.gpsimd.tensor_scalar(
-                out=st[("eg", u)][:, i, :, :],
-                in0=st[("ep", u, h)][:, ii, :, :].rearrange("p j q -> p q j"),
+                out=st[("eg", u)][:, 2 * h : 2 * h + 2, :, :],
+                in0=st[("ep", u, h)][:].rearrange("p i j q -> p i q j"),
                 scalar1=1.0,
                 scalar2=0.0,
                 op0=ALU.mult,
@@ -291,14 +289,12 @@ def tile_localselfattention_kernel(tc, Q, K, V, mask, out):
                 if ok(u + 2) and (u + 2) % GROUP == GROUP - 1:
                     load_group((u + 2) // GROUP + LOAD_BUFS)
             if i == 0:
-                gp_e_regroup(u - 2, 2)
+                gp_e_regroup(u - 2, 1)
             elif i == 1:
-                gp_e_regroup(u - 2, 3)
-                gp_v_regroup(u + 5)
+                if (u + 5) % GROUP == 0:
+                    gp_v_regroup((u + 5) // GROUP)
             elif i == 2:
                 gp_e_regroup(u - 1, 0)
-            else:
-                gp_e_regroup(u - 1, 1)
             um, im = divmod(s - 1, 4)
             ve_max(um, im)
             if i == 0:

@@ -40,6 +40,7 @@ def tile_localselfattention_kernel(tc, Q, K, V, mask, out):
         vpool = ctx.enter_context(tc.tile_pool(name="vpool", bufs=3))
         work = ctx.enter_context(tc.tile_pool(name="work", bufs=3))
         stat = ctx.enter_context(tc.tile_pool(name="stat", bufs=8))
+        spool = ctx.enter_context(tc.tile_pool(name="spool", bufs=5))
         ps_t = ctx.enter_context(tc.psum_pool(name="ps_t", bufs=1))
         ps_s = ctx.enter_context(tc.psum_pool(name="ps_s", bufs=4))
         ps_e = ctx.enter_context(tc.psum_pool(name="ps_e", bufs=2))
@@ -199,10 +200,18 @@ def tile_localselfattention_kernel(tc, Q, K, V, mask, out):
             if not ok(u):
                 return
             negm = stat.tile([P, 1], F32, name="negm", tag="negm")
-            nc.vector.tensor_reduce(
-                out=negm[:], in_=st[("s_ps", u, i)][:], axis=AX.X, op=ALU.max, negate=True
+            sneg = spool.tile([P, BS], F32, name="sneg", tag="sneg")
+            nc.vector.tensor_scalar(
+                out=sneg[:],
+                in0=st[("s_ps", u, i)][:],
+                scalar1=-1.0,
+                scalar2=None,
+                op0=ALU.mult,
+                op1=ALU.min,
+                accum_out=negm[:],
             )
             st[("negm", u, i)] = negm
+            st[("sneg", u, i)] = sneg
 
         def ve_v_quantise(vb):
             if not 0 <= vb < UNITS // VBATCH:
@@ -261,10 +270,10 @@ def tile_localselfattention_kernel(tc, Q, K, V, mask, out):
                 st[("e_sb", u, h)] = work.tile([P, 2, BS], BF16, name="e_sb", tag="e_sb")
             nc.scalar.activation(
                 out=st[("e_sb", u, h)][:, ii, :],
-                in_=st[("s_ps", u, i)][:],
+                in_=st[("sneg", u, i)][:],
                 func=ACT.Exp,
                 bias=st[("negm", u, i)][:],
-                scale=1.0,
+                scale=-1.0,
                 accum_out=st[("rsum", u)][:, i : i + 1],
             )
 
@@ -275,40 +284,40 @@ def tile_localselfattention_kernel(tc, Q, K, V, mask, out):
             nc.scalar.copy(out=ep[:], in_=st[("eT_ps", u, h)][:])
             st[("ep", u, h)] = ep
 
-        for s in range(-20, 4 * UNITS + 16):
+        for s in range(-20, 4 * UNITS + 20):
             u, i = divmod(s, 4)
             pe_scores(u, i)
             if i == 0:
-                pe_e_transposes(u - 1, 0)
+                pe_e_transposes(u - 2, 1)
             elif i == 1:
-                pe_pv(u - 3)
+                pe_pv(u - 4)
             elif i == 2:
-                pe_e_transposes(u - 1, 1)
+                pe_e_transposes(u - 1, 0)
             else:
                 pe_qk_transposes(u + 2)
                 if ok(u + 2) and (u + 2) % GROUP == GROUP - 1:
                     load_group((u + 2) // GROUP + LOAD_BUFS)
             if i == 0:
-                gp_e_regroup(u - 2, 1)
-            elif i == 1:
                 if (u + 5) % GROUP == 0:
                     gp_v_regroup((u + 5) // GROUP)
-            elif i == 2:
-                gp_e_regroup(u - 1, 0)
-            um, im = divmod(s - 1, 4)
+            elif i == 1:
+                gp_e_regroup(u - 2, 0)
+            elif i == 3:
+                gp_e_regroup(u - 2, 1)
+            um, im = divmod(s - 2, 4)
             ve_max(um, im)
             if i == 0:
                 if (u + 1) % VBATCH == 0:
                     ve_v_quantise((u + 1) // VBATCH)
             elif i == 2:
-                ve_out(u - 3)
+                ve_e_quantise(u - 3)
             elif i == 3:
-                ve_e_quantise(u - 2)
-            ux, ix = divmod(s - 2, 4)
+                ve_out(u - 4)
+            ux, ix = divmod(s - 4, 4)
             se_exp(ux, ix)
             if i == 0:
-                se_qk_copy(u + 1)
+                se_e_copy(u - 2, 0)
             elif i == 1:
-                se_e_copy(u - 1, 0)
-            elif i == 3:
-                se_e_copy(u - 1, 1)
+                se_qk_copy(u + 1)
+            elif i == 2:
+                se_e_copy(u - 2, 1)

@@ -56,15 +56,24 @@ def tile_localselfattention_kernel(tc, Q, K, V, mask, out):
             tiles = []
             for src, tag in ((qf, "q_raw"), (kf, "k_raw"), (vf, "v_raw")):
                 t_raw = loads.tile([P, GROUP, T, D], BF16, name=tag, tag=tag)
-                nc.sync.dma_start(
-                    out=t_raw[:], in_=src[rows, :].rearrange("(u p t) d -> p u t d", p=P, t=T)
-                )
+                if tag == "k_raw":
+                    nc.sync.dma_start(
+                        out=t_raw[:].rearrange("x g (h w) d -> x (g h) (w d)", w=2),
+                        in_=src[rows, :].rearrange("(gh x w) d -> x gh (w d)", x=P, w=2),
+                    )
+                else:
+                    nc.sync.dma_start(
+                        out=t_raw[:], in_=src[rows, :].rearrange("(u p t) d -> p u t d", p=P, t=T)
+                    )
                 tiles.append(t_raw)
             raw[g] = tiles
 
         mk = const.tile([P, B, NB, T], BF16, name="mk")
         with nc.allow_non_contiguous_dma(reason="the mask, four positions to a partition"):
             nc.sync.dma_start(out=mk[:], in_=mask.rearrange("b (n p t) -> p b n t", p=P, t=T))
+        mkk = const.tile([P, B, NB * 2, 2], BF16, name="mkk")
+        with nc.allow_non_contiguous_dma(reason="the mask, two positions to a piece"):
+            nc.sync.dma_start(out=mkk[:], in_=mask.rearrange("b (nh x w) -> x b nh w", x=P, w=2))
         for g in range(LOAD_BUFS):
             load_group(g)
 
@@ -76,19 +85,17 @@ def tile_localselfattention_kernel(tc, Q, K, V, mask, out):
         mkf = mk[:].rearrange("p b n t -> p (b n t)")
         bcol = const.tile([P, NM], F32, name="bcol")
         nc.vector.tensor_scalar(
-            out=bcol[:], in0=mkf, scalar1=0.0, scalar2=NEG, op0=ALU.is_equal, op1=ALU.mult
+            out=bcol[:],
+            in0=mkk[:].rearrange("p b a w -> p (b a w)"),
+            scalar1=0.0,
+            scalar2=NEG,
+            op0=ALU.is_equal,
+            op1=ALU.mult,
         )
         bt = const.tile([P, NM, P], F32, name="bt")
         nc.vector.tensor_copy(out=bt[:], in_=bcol[:].unsqueeze(2).to_broadcast([P, NM, P]))
-        keepq = const.tile([P, NM], BF16, name="keepq")
+        keepq = const.tile([P, NM], F32, name="keepq")
         nc.vector.tensor_single_scalar(out=keepq[:], in_=mkf, scalar=0.0, op=ALU.not_equal)
-        dq = const.tile([P, NM, P], BF16, name="dq")
-        nc.vector.tensor_tensor(
-            out=dq[:],
-            in0=ident_bf[:].unsqueeze(1).to_broadcast([P, NM, P]),
-            in1=keepq[:].unsqueeze(2).to_broadcast([P, NM, P]),
-            op=ALU.mult,
-        )
 
         def ok(u):
             return 0 <= u < UNITS
@@ -104,7 +111,8 @@ def tile_localselfattention_kernel(tc, Q, K, V, mask, out):
             for t in range(T):
                 nc.tensor.transpose(qkT_ps[:, t, :], raw[g][0][:, ul, t, :], ident_bf[:])
             for t in range(T):
-                nc.tensor.transpose(qkT_ps[:, T + t, :], raw[g][1][:, ul, t, :], ident_bf[:])
+                h, w = divmod(t, 2)
+                nc.tensor.transpose(qkT_ps[:, T + 2 * w + h, :], raw[g][1][:, ul, t, :], ident_bf[:])
             st[("qkT_ps", u)] = qkT_ps
 
         def pe_scores(u, i):
@@ -114,9 +122,10 @@ def tile_localselfattention_kernel(tc, Q, K, V, mask, out):
             qkT = st[("qkT", u)]
             s_ps = ps_s.tile([P, BS], F32, name="s_ps", tag="s_ps")
             for t in range(T):
+                w, h = divmod(t, 2)
                 nc.tensor.matmul(
                     out=s_ps[:, t * P : (t + 1) * P],
-                    lhsT=bt[:, mg * T + t, :],
+                    lhsT=bt[:, mg * T + 2 * h + w, :],
                     rhs=ident_f[:],
                     is_transpose=True,
                     start=(t == 0),
@@ -134,15 +143,15 @@ def tile_localselfattention_kernel(tc, Q, K, V, mask, out):
         def pe_e_transposes(u, h):
             if not ok(u):
                 return
-            mg = mask_group(u)
             e_sb = st[("e_sb", u, h)]
-            eT_ps = ps_e.tile([P, 2, T, P], BF16, name="eT_ps", tag="eT_ps")
+            eT_ps = ps_e.tile([P, 2, 2, P], F32, name="eT_ps", tag="eT_ps")
             for ii in range(2):
-                for j in range(T):
+                words = e_sb[:, ii, :].bitcast(F32)
+                for w in range(2):
                     nc.tensor.transpose(
-                        eT_ps[:, ii, j, :],
-                        e_sb[:, ii, j * P : (j + 1) * P],
-                        dq[:, mg * T + 2 * h + ii, :],
+                        eT_ps[:, ii, w, :],
+                        words[:, w * P : (w + 1) * P],
+                        ident_f[:],
                     )
             st[("eT_ps", u, h)] = eT_ps
 
@@ -173,28 +182,15 @@ def tile_localselfattention_kernel(tc, Q, K, V, mask, out):
                 st[("vg", vb)] = vpool.tile(
                     [P, VBATCH, D, T], BF16, name="vg", tag="vg", align_bytes=64
                 )
-            nc.gpsimd.tensor_scalar(
-                out=st[("vg", vb)][:, vl : vl + GROUP, :, :],
-                in0=raw[g][2][:].rearrange("p u j d -> p u d j"),
-                scalar1=1.0,
-                scalar2=0.0,
-                op0=ALU.mult,
-                op1=ALU.add,
-            )
-
-        def gp_e_regroup(u, h):
-            if not ok(u):
-                return
-            if h == 0:
-                st[("eg", u)] = work.tile([P, T, P, T], BF16, name="eg", tag="eg", align_bytes=64)
-            nc.gpsimd.tensor_scalar(
-                out=st[("eg", u)][:, 2 * h : 2 * h + 2, :, :],
-                in0=st[("ep", u, h)][:].rearrange("p i j q -> p i q j"),
-                scalar1=1.0,
-                scalar2=0.0,
-                op0=ALU.mult,
-                op1=ALU.add,
-            )
+            for ul in range(GROUP):
+                nc.gpsimd.tensor_scalar(
+                    out=st[("vg", vb)][:, vl + ul, :, :].rearrange("p d (w e) -> p d w e", e=2),
+                    in0=raw[g][2][:, ul, :, :].rearrange("p (e w) d -> p d w e", w=2),
+                    scalar1=1.0,
+                    scalar2=0.0,
+                    op0=ALU.mult,
+                    op1=ALU.add,
+                )
 
         def ve_max(u, i):
             if not ok(u):
@@ -233,7 +229,7 @@ def tile_localselfattention_kernel(tc, Q, K, V, mask, out):
             nc.vector.quantize_mx(
                 out=ecodes[:].bitcast(FP8X4),
                 scales=escales[:],
-                in_=st[("eg", u)][:].rearrange("p i q j -> p (i q j)"),
+                in_=st[("eg", u)][:],
             )
             st[("eq", u)] = (ecodes, escales)
 
@@ -242,6 +238,10 @@ def tile_localselfattention_kernel(tc, Q, K, V, mask, out):
                 return
             rinv = stat.tile([P, T], F32, name="rinv", tag="rinv")
             nc.vector.reciprocal(out=rinv[:], in_=st[("rsum", u)][:])
+            mg = mask_group(u)
+            nc.vector.tensor_tensor(
+                out=rinv[:], in0=rinv[:], in1=keepq[:, mg * T : (mg + 1) * T], op=ALU.mult
+            )
             o_sb = work.tile([P, T, D], F32, name="o_sb", tag="o_sb")
             nc.vector.tensor_tensor(
                 out=o_sb[:],
@@ -280,9 +280,15 @@ def tile_localselfattention_kernel(tc, Q, K, V, mask, out):
         def se_e_copy(u, h):
             if not ok(u):
                 return
-            ep = work.tile([P, 2, T, P], BF16, name="ep", tag="ep")
-            nc.scalar.copy(out=ep[:], in_=st[("eT_ps", u, h)][:])
-            st[("ep", u, h)] = ep
+            if h == 0:
+                st[("eg", u)] = work.tile([P, T * P * T], BF16, name="eg", tag="eg", align_bytes=64)
+            half = T * P * T // 2
+            nc.scalar.copy(
+                out=st[("eg", u)][:, h * half : (h + 1) * half]
+                .bitcast(F32)
+                .rearrange("p (i q w) -> p i q w", i=2, w=2),
+                in_=st[("eT_ps", u, h)][:].rearrange("p i w q -> p i q w"),
+            )
 
         for s in range(-20, 4 * UNITS + 20):
             u, i = divmod(s, 4)
@@ -300,10 +306,6 @@ def tile_localselfattention_kernel(tc, Q, K, V, mask, out):
             if i == 0:
                 if (u + 5) % GROUP == 0:
                     gp_v_regroup((u + 5) // GROUP)
-            elif i == 1:
-                gp_e_regroup(u - 2, 0)
-            elif i == 3:
-                gp_e_regroup(u - 2, 1)
             um, im = divmod(s - 2, 4)
             ve_max(um, im)
             if i == 0:

@@ -192,6 +192,19 @@ def tile_localselfattention_kernel(tc, Q, K, V, mask, out):
                     op1=ALU.add,
                 )
 
+        def gp_keep(u):
+            if not ok(u):
+                return
+            mg = mask_group(u)
+            rkeep = stat.tile([P, T], F32, name="rkeep", tag="rkeep")
+            nc.gpsimd.tensor_tensor(
+                out=rkeep[:],
+                in0=st[("rinv", u)][:],
+                in1=keepq[:, mg * T : (mg + 1) * T],
+                op=ALU.mult,
+            )
+            st[("rkeep", u)] = rkeep
+
         def ve_max(u, i):
             if not ok(u):
                 return
@@ -233,20 +246,21 @@ def tile_localselfattention_kernel(tc, Q, K, V, mask, out):
             )
             st[("eq", u)] = (ecodes, escales)
 
-        def ve_out(u):
+        def ve_recip(u):
             if not ok(u):
                 return
             rinv = stat.tile([P, T], F32, name="rinv", tag="rinv")
             nc.vector.reciprocal(out=rinv[:], in_=st[("rsum", u)][:])
-            mg = mask_group(u)
-            nc.vector.tensor_tensor(
-                out=rinv[:], in0=rinv[:], in1=keepq[:, mg * T : (mg + 1) * T], op=ALU.mult
-            )
+            st[("rinv", u)] = rinv
+
+        def ve_out(u):
+            if not ok(u):
+                return
             o_sb = work.tile([P, T, D], F32, name="o_sb", tag="o_sb")
             nc.vector.tensor_tensor(
                 out=o_sb[:],
                 in0=st[("pv_ps", u)][:],
-                in1=rinv[:].unsqueeze(2).to_broadcast([P, T, D]),
+                in1=st[("rkeep", u)][:].unsqueeze(2).to_broadcast([P, T, D]),
                 op=ALU.mult,
             )
             nc.sync.dma_start(
@@ -306,11 +320,15 @@ def tile_localselfattention_kernel(tc, Q, K, V, mask, out):
             if i == 0:
                 if (u + 5) % GROUP == 0:
                     gp_v_regroup((u + 5) // GROUP)
+            elif i == 3:
+                gp_keep(u - 3)
             um, im = divmod(s - 2, 4)
             ve_max(um, im)
             if i == 0:
                 if (u + 1) % VBATCH == 0:
                     ve_v_quantise((u + 1) // VBATCH)
+            elif i == 1:
+                ve_recip(u - 3)
             elif i == 2:
                 ve_e_quantise(u - 3)
             elif i == 3:

@@ -40,7 +40,6 @@ def tile_localselfattention_kernel(tc, Q, K, V, mask, out):
         vpool = ctx.enter_context(tc.tile_pool(name="vpool", bufs=3))
         work = ctx.enter_context(tc.tile_pool(name="work", bufs=3))
         stat = ctx.enter_context(tc.tile_pool(name="stat", bufs=8))
-        spool = ctx.enter_context(tc.tile_pool(name="spool", bufs=5))
         ps_t = ctx.enter_context(tc.psum_pool(name="ps_t", bufs=1))
         ps_s = ctx.enter_context(tc.psum_pool(name="ps_s", bufs=4))
         ps_e = ctx.enter_context(tc.psum_pool(name="ps_e", bufs=2))
@@ -209,18 +208,10 @@ def tile_localselfattention_kernel(tc, Q, K, V, mask, out):
             if not ok(u):
                 return
             negm = stat.tile([P, 1], F32, name="negm", tag="negm")
-            sneg = spool.tile([P, BS], F32, name="sneg", tag="sneg")
-            nc.vector.tensor_scalar(
-                out=sneg[:],
-                in0=st[("s_ps", u, i)][:],
-                scalar1=-1.0,
-                scalar2=None,
-                op0=ALU.mult,
-                op1=ALU.min,
-                accum_out=negm[:],
+            nc.vector.tensor_reduce(
+                out=negm[:], in_=st[("s_ps", u, i)][:], axis=AX.X, op=ALU.max, negate=True
             )
             st[("negm", u, i)] = negm
-            st[("sneg", u, i)] = sneg
 
         def ve_v_quantise(vb):
             if not 0 <= vb < UNITS // VBATCH:
@@ -284,10 +275,10 @@ def tile_localselfattention_kernel(tc, Q, K, V, mask, out):
                 st[("e_sb", u, h)] = work.tile([P, 2, BS], BF16, name="e_sb", tag="e_sb")
             nc.scalar.activation(
                 out=st[("e_sb", u, h)][:, ii, :],
-                in_=st[("sneg", u, i)][:],
+                in_=st[("s_ps", u, i)][:],
                 func=ACT.Exp,
                 bias=st[("negm", u, i)][:],
-                scale=-1.0,
+                scale=1.0,
                 accum_out=st[("rsum", u)][:, i : i + 1],
             )
 
@@ -322,7 +313,7 @@ def tile_localselfattention_kernel(tc, Q, K, V, mask, out):
                     gp_v_regroup((u + 5) // GROUP)
             elif i == 3:
                 gp_keep(u - 3)
-            um, im = divmod(s - 2, 4)
+            um, im = divmod(s - 1, 4)
             ve_max(um, im)
             if i == 0:
                 if (u + 1) % VBATCH == 0:
@@ -333,7 +324,7 @@ def tile_localselfattention_kernel(tc, Q, K, V, mask, out):
                 ve_e_quantise(u - 3)
             elif i == 3:
                 ve_out(u - 4)
-            ux, ix = divmod(s - 4, 4)
+            ux, ix = divmod(s - 2, 4)
             se_exp(ux, ix)
             if i == 0:
                 se_e_copy(u - 2, 0)

@@ -258,11 +258,14 @@ def tile_localselfattention_kernel(tc, Q, K, V, mask, out):
                 out=of[u * BS : (u + 1) * BS, :].rearrange("(p t) d -> p t d", t=T), in_=o_sb[:]
             )
 
-        def se_qk_copy(u):
-            if not ok(u):
+        def qk_copy(u, on_vector):
+            if not ok(u) or (u % 2 == 1) != on_vector:
                 return
             qkT = work.tile([P, 2 * T, P], BF16, name="qkT", tag="qkT")
-            nc.scalar.copy(out=qkT[:], in_=st[("qkT_ps", u)][:])
+            if on_vector:
+                nc.vector.tensor_copy(out=qkT[:], in_=st[("qkT_ps", u)][:])
+            else:
+                nc.scalar.copy(out=qkT[:], in_=st[("qkT_ps", u)][:])
             st[("qkT", u)] = qkT
 
         def se_exp(u, i):
@@ -320,6 +323,7 @@ def tile_localselfattention_kernel(tc, Q, K, V, mask, out):
                     ve_v_quantise((u + 1) // VBATCH)
             elif i == 1:
                 ve_recip(u - 3)
+                qk_copy(u + 1, True)
             elif i == 2:
                 ve_e_quantise(u - 3)
             elif i == 3:
@@ -329,6 +333,6 @@ def tile_localselfattention_kernel(tc, Q, K, V, mask, out):
             if i == 0:
                 se_e_copy(u - 2, 0)
             elif i == 1:
-                se_qk_copy(u + 1)
+                qk_copy(u + 1, False)
             elif i == 2:
                 se_e_copy(u - 2, 1)

@@ -55,7 +55,7 @@ def tile_localselfattention_kernel(tc, Q, K, V, mask, out):
             tiles = []
             for src, tag in ((qf, "q_raw"), (kf, "k_raw"), (vf, "v_raw")):
                 t_raw = loads.tile([P, GROUP, T, D], BF16, name=tag, tag=tag)
-                if tag == "k_raw":
+                if tag == "q_raw":
                     nc.sync.dma_start(
                         out=t_raw[:].rearrange("x g (h w) d -> x (g h) (w d)", w=2),
                         in_=src[rows, :].rearrange("(gh x w) d -> x gh (w d)", x=P, w=2),
@@ -67,13 +67,14 @@ def tile_localselfattention_kernel(tc, Q, K, V, mask, out):
                 tiles.append(t_raw)
             raw[g] = tiles
 
-        mk = const.tile([P, B, NB, T], BF16, name="mk")
-        with nc.allow_non_contiguous_dma(reason="the mask, four positions to a partition"):
-            nc.sync.dma_start(out=mk[:], in_=mask.rearrange("b (n p t) -> p b n t", p=P, t=T))
         mkk = const.tile([P, B, NB * 2, 2], BF16, name="mkk")
         with nc.allow_non_contiguous_dma(reason="the mask, two positions to a piece"):
             nc.sync.dma_start(out=mkk[:], in_=mask.rearrange("b (nh x w) -> x b nh w", x=P, w=2))
-        for g in range(LOAD_BUFS):
+        load_group(0)
+        mrow = const.tile([P, P], BF16, name="mrow")
+        nc.vector.memset(mrow[:], 0.0)
+        nc.sync.dma_start(out=mrow[0:NM, :], in_=mask.rearrange("b (n t p) -> (b n t) p", t=T, p=P))
+        for g in range(1, LOAD_BUFS):
             load_group(g)
 
         ident_bf = const.tile([P, P], BF16, name="ident_bf")
@@ -81,7 +82,6 @@ def tile_localselfattention_kernel(tc, Q, K, V, mask, out):
         ident_f = const.tile([P, P], F32, name="ident_f")
         make_identity(nc, ident_f[:])
 
-        mkf = mk[:].rearrange("p b n t -> p (b n t)")
         bcol = const.tile([P, NM], F32, name="bcol")
         nc.vector.tensor_scalar(
             out=bcol[:],
@@ -94,7 +94,9 @@ def tile_localselfattention_kernel(tc, Q, K, V, mask, out):
         bt = const.tile([P, NM, P], F32, name="bt")
         nc.vector.tensor_copy(out=bt[:], in_=bcol[:].unsqueeze(2).to_broadcast([P, NM, P]))
         keepq = const.tile([P, NM], F32, name="keepq")
-        nc.vector.tensor_single_scalar(out=keepq[:], in_=mkf, scalar=0.0, op=ALU.not_equal)
+        kq_ps = ps_o.tile([P, P], BF16, name="kq_ps", tag="pv_ps")
+        nc.tensor.transpose(kq_ps[:], mrow[:], ident_bf[:])
+        nc.vector.tensor_single_scalar(out=keepq[:], in_=kq_ps[:, 0:NM], scalar=0.0, op=ALU.not_equal)
 
         def ok(u):
             return 0 <= u < UNITS
@@ -105,13 +107,14 @@ def tile_localselfattention_kernel(tc, Q, K, V, mask, out):
         def pe_qk_transposes(u):
             if not ok(u):
                 return
-            g, ul = divmod(u, GROUP)
-            qkT_ps = ps_t.tile([P, 2 * T, P], BF16, name="qkT_ps", tag="qkT_ps")
-            for t in range(T):
-                nc.tensor.transpose(qkT_ps[:, t, :], raw[g][0][:, ul, t, :], ident_bf[:])
-            for t in range(T):
-                h, w = divmod(t, 2)
-                nc.tensor.transpose(qkT_ps[:, T + 2 * w + h, :], raw[g][1][:, ul, t, :], ident_bf[:])
+            qki = st[("qki", u)]
+            qkT_ps = ps_t.tile([P, T, P], F32, name="qkT_ps", tag="qkT_ps")
+            for c in range(T):
+                nc.tensor.transpose(
+                    qkT_ps[:, c, :],
+                    qki[:, c, :, :].rearrange("p d e -> p (d e)").bitcast(F32),
+                    ident_f[:],
+                )
             st[("qkT_ps", u)] = qkT_ps
 
         def pe_scores(u, i):
@@ -132,8 +135,8 @@ def tile_localselfattention_kernel(tc, Q, K, V, mask, out):
                 )
             nc.tensor.matmul(
                 out=s_ps[:],
-                lhsT=qkT[:, i, :],
-                rhs=qkT[:, T : 2 * T, :].rearrange("p t k -> p (t k)"),
+                lhsT=qkT[:, i * P : (i + 1) * P],
+                rhs=qkT[:, BS : 2 * BS],
                 start=False,
                 stop=True,
             )
@@ -173,23 +176,31 @@ def tile_localselfattention_kernel(tc, Q, K, V, mask, out):
                 )
             st[("pv_ps", u)] = pv_ps
 
-        def gp_v_regroup(g):
-            if not 0 <= g < NGROUPS:
+        def gp_copy(out, in0):
+            nc.gpsimd.tensor_scalar(out=out, in0=in0, scalar1=1.0, scalar2=0.0, op0=ALU.mult, op1=ALU.add)
+
+        def gp_v_regroup(u):
+            if not ok(u):
                 return
-            vb, vl = divmod(g * GROUP, VBATCH)
+            g, ul = divmod(u, GROUP)
+            vb, vl = divmod(u, VBATCH)
             if vl == 0:
                 st[("vg", vb)] = vpool.tile(
                     [P, VBATCH, D, T], BF16, name="vg", tag="vg", align_bytes=64
                 )
-            for ul in range(GROUP):
-                nc.gpsimd.tensor_scalar(
-                    out=st[("vg", vb)][:, vl + ul, :, :].rearrange("p d (w e) -> p d w e", e=2),
-                    in0=raw[g][2][:, ul, :, :].rearrange("p (e w) d -> p d w e", w=2),
-                    scalar1=1.0,
-                    scalar2=0.0,
-                    op0=ALU.mult,
-                    op1=ALU.add,
-                )
+            gp_copy(
+                st[("vg", vb)][:, vl, :, :].rearrange("p d (w e) -> p d w e", e=2),
+                raw[g][2][:, ul, :, :].rearrange("p (e w) d -> p d w e", w=2),
+            )
+
+        def gp_qk_pairs(u):
+            if not ok(u):
+                return
+            g, ul = divmod(u, GROUP)
+            qki = work.tile([P, T, D, 2], BF16, name="qki", tag="qki")
+            gp_copy(qki[:, 0:2, :, :], raw[g][0][:, ul, :, :].rearrange("p (j e) d -> p j d e", e=2))
+            gp_copy(qki[:, 2:4, :, :], raw[g][1][:, ul, :, :].rearrange("p (e w) d -> p w d e", w=2))
+            st[("qki", u)] = qki
 
         def gp_keep(u):
             if not ok(u):
@@ -255,17 +266,18 @@ def tile_localselfattention_kernel(tc, Q, K, V, mask, out):
                 op=ALU.mult,
             )
             nc.sync.dma_start(
-                out=of[u * BS : (u + 1) * BS, :].rearrange("(p t) d -> p t d", t=T), in_=o_sb[:]
+                out=of[u * BS : (u + 1) * BS, :].rearrange("(t p) d -> p t d", p=P), in_=o_sb[:]
             )
 
         def qk_copy(u, on_vector):
             if not ok(u) or (u % 2 == 1) != on_vector:
                 return
-            qkT = work.tile([P, 2 * T, P], BF16, name="qkT", tag="qkT")
+            qkT = work.tile([P, 2 * BS], BF16, name="qkT", tag="qkT")
+            words = st[("qkT_ps", u)][:].rearrange("p c x -> p (c x)")
             if on_vector:
-                nc.vector.tensor_copy(out=qkT[:], in_=st[("qkT_ps", u)][:])
+                nc.vector.tensor_copy(out=qkT[:].bitcast(F32), in_=words)
             else:
-                nc.scalar.copy(out=qkT[:], in_=st[("qkT_ps", u)][:])
+                nc.scalar.copy(out=qkT[:].bitcast(F32), in_=words)
             st[("qkT", u)] = qkT
 
         def se_exp(u, i):
@@ -309,25 +321,23 @@ def tile_localselfattention_kernel(tc, Q, K, V, mask, out):
                 pe_e_transposes(u - 1, 0)
             else:
                 pe_qk_transposes(u + 2)
-                if ok(u + 2) and (u + 2) % GROUP == GROUP - 1:
-                    load_group((u + 2) // GROUP + LOAD_BUFS)
-            if i == 0:
-                if (u + 5) % GROUP == 0:
-                    gp_v_regroup((u + 5) // GROUP)
-            elif i == 3:
-                gp_keep(u - 3)
             um, im = divmod(s - 1, 4)
             ve_max(um, im)
-            if i == 0:
-                if (u + 1) % VBATCH == 0:
-                    ve_v_quantise((u + 1) // VBATCH)
-            elif i == 1:
-                ve_recip(u - 3)
+            if i == 1:
                 qk_copy(u + 1, True)
             elif i == 2:
+                if (u - 2) % VBATCH == 0:
+                    ve_v_quantise((u - 2) // VBATCH)
                 ve_e_quantise(u - 3)
+                ve_recip(u - 2)
             elif i == 3:
                 ve_out(u - 4)
+            if i == 2:
+                gp_keep(u - 2)
+                gp_qk_pairs(u + 4)
+                gp_v_regroup(u + 2)
+                if ok(u + 2) and (u + 2) % GROUP == GROUP - 1:
+                    load_group((u + 2) // GROUP + LOAD_BUFS)
             ux, ix = divmod(s - 2, 4)
             se_exp(ux, ix)
             if i == 0:

@@ -40,10 +40,8 @@ def tile_localselfattention_kernel(tc, Q, K, V, mask, out):
         vpool = ctx.enter_context(tc.tile_pool(name="vpool", bufs=3))
         work = ctx.enter_context(tc.tile_pool(name="work", bufs=3))
         stat = ctx.enter_context(tc.tile_pool(name="stat", bufs=8))
-        ps_t = ctx.enter_context(tc.psum_pool(name="ps_t", bufs=1))
-        ps_s = ctx.enter_context(tc.psum_pool(name="ps_s", bufs=4))
-        ps_e = ctx.enter_context(tc.psum_pool(name="ps_e", bufs=2))
-        ps_o = ctx.enter_context(tc.psum_pool(name="ps_o", bufs=1))
+        ps_s = ctx.enter_context(tc.psum_pool(name="ps_s", bufs=5))
+        ps_x = ctx.enter_context(tc.psum_pool(name="ps_x", bufs=3))
 
         raw = {}
         st = {}
@@ -94,7 +92,7 @@ def tile_localselfattention_kernel(tc, Q, K, V, mask, out):
         bt = const.tile([P, NM, P], F32, name="bt")
         nc.vector.tensor_copy(out=bt[:], in_=bcol[:].unsqueeze(2).to_broadcast([P, NM, P]))
         keepq = const.tile([P, NM], F32, name="keepq")
-        kq_ps = ps_o.tile([P, P], BF16, name="kq_ps", tag="pv_ps")
+        kq_ps = ps_x.tile([P, P], BF16, name="kq_ps", tag="aux")
         nc.tensor.transpose(kq_ps[:], mrow[:], ident_bf[:])
         nc.vector.tensor_single_scalar(out=keepq[:], in_=kq_ps[:, 0:NM], scalar=0.0, op=ALU.not_equal)
 
@@ -108,7 +106,7 @@ def tile_localselfattention_kernel(tc, Q, K, V, mask, out):
             if not ok(u):
                 return
             qki = st[("qki", u)]
-            qkT_ps = ps_t.tile([P, T, P], F32, name="qkT_ps", tag="qkT_ps")
+            qkT_ps = ps_x.tile([P, T, P], F32, name="qkT_ps", tag="aux")
             for c in range(T):
                 nc.tensor.transpose(
                     qkT_ps[:, c, :],
@@ -146,7 +144,7 @@ def tile_localselfattention_kernel(tc, Q, K, V, mask, out):
             if not ok(u):
                 return
             e_sb = st[("e_sb", u, h)]
-            eT_ps = ps_e.tile([P, 2, 2, P], F32, name="eT_ps", tag="eT_ps")
+            eT_ps = ps_x.tile([P, 2, 2, P], F32, name="eT_ps", tag="aux")
             for ii in range(2):
                 words = e_sb[:, ii, :].bitcast(F32)
                 for w in range(2):
@@ -163,7 +161,7 @@ def tile_localselfattention_kernel(tc, Q, K, V, mask, out):
             ecodes, escales = st[("eq", u)]
             vcodes, vscales = st[("vq", u // VBATCH)]
             cols = slice((u % VBATCH) * D, (u % VBATCH + 1) * D)
-            pv_ps = ps_o.tile([P, T, D], F32, name="pv_ps", tag="pv_ps")
+            pv_ps = ps_x.tile([P, T, D], F32, name="pv_ps", tag="aux")
             for i in range(T):
                 nc.tensor.matmul_mx(
                     out=pv_ps[:, i, :],
@@ -314,35 +312,35 @@ def tile_localselfattention_kernel(tc, Q, K, V, mask, out):
             u, i = divmod(s, 4)
             pe_scores(u, i)
             if i == 0:
-                pe_e_transposes(u - 2, 1)
-            elif i == 1:
                 pe_pv(u - 4)
+            elif i == 1:
+                pe_e_transposes(u - 2, 1)
             elif i == 2:
-                pe_e_transposes(u - 1, 0)
-            else:
                 pe_qk_transposes(u + 2)
-            um, im = divmod(s - 1, 4)
+            else:
+                pe_e_transposes(u - 1, 0)
+            um, im = divmod(s - 2, 4)
             ve_max(um, im)
-            if i == 1:
+            if i == 0:
                 qk_copy(u + 1, True)
-            elif i == 2:
+            elif i == 1:
                 if (u - 2) % VBATCH == 0:
                     ve_v_quantise((u - 2) // VBATCH)
                 ve_e_quantise(u - 3)
                 ve_recip(u - 2)
-            elif i == 3:
+            elif i == 2:
                 ve_out(u - 4)
-            if i == 2:
+            if i == 1:
                 gp_keep(u - 2)
                 gp_qk_pairs(u + 4)
                 gp_v_regroup(u + 2)
                 if ok(u + 2) and (u + 2) % GROUP == GROUP - 1:
                     load_group((u + 2) // GROUP + LOAD_BUFS)
-            ux, ix = divmod(s - 2, 4)
+            ux, ix = divmod(s - 4, 4)
             se_exp(ux, ix)
             if i == 0:
-                se_e_copy(u - 2, 0)
-            elif i == 1:
                 qk_copy(u + 1, False)
-            elif i == 2:
+            elif i == 1:
+                se_e_copy(u - 2, 0)
+            elif i == 3:
                 se_e_copy(u - 2, 1)

@@ -17,11 +17,13 @@ B, H, S, D, BS = 2, 12, 1024, 128, 512
 NB = S // BS
 UNITS = B * H * NB
 T = BS // P
-GROUP = 2
+GROUP = 1
 VBATCH = 4
 NGROUPS = UNITS // GROUP
-LOAD_BUFS = 4
+LOAD_BUFS = 8
 NEG = -10000.0
+NWARM = 6
+LAST = UNITS - 1
 FLOPS = 2 * 2 * BS * BS * D * UNITS
 
 
@@ -67,18 +69,23 @@ def tile_localselfattention_kernel(tc, Q, K, V, mask, out):
 
         mkk = const.tile([P, B, NB * 2, 2], BF16, name="mkk")
         with nc.allow_non_contiguous_dma(reason="the mask, two positions to a piece"):
-            nc.sync.dma_start(out=mkk[:], in_=mask.rearrange("b (nh x w) -> x b nh w", x=P, w=2))
+            nc.scalar.dma_start(out=mkk[:], in_=mask.rearrange("b (nh x w) -> x b nh w", x=P, w=2))
         load_group(0)
+        warm = const.tile([P, BS], BF16, name="warm")
+        nc.vector.memset(warm[:], 0.0)
+        for k in range(NWARM):
+            w_ps = ps_s.tile([P, BS], F32, name="w_ps", tag="s_ps")
+            nc.tensor.matmul(out=w_ps[:], lhsT=warm[:, 0:P], rhs=warm[:], start=True, stop=True)
         mrow = const.tile([P, P], BF16, name="mrow")
         nc.vector.memset(mrow[:], 0.0)
         nc.sync.dma_start(out=mrow[0:NM, :], in_=mask.rearrange("b (n t p) -> (b n t) p", t=T, p=P))
         for g in range(1, LOAD_BUFS):
             load_group(g)
 
-        ident_bf = const.tile([P, P], BF16, name="ident_bf")
-        make_identity(nc, ident_bf[:])
         ident_f = const.tile([P, P], F32, name="ident_f")
         make_identity(nc, ident_f[:])
+        ident_bf = const.tile([P, P], BF16, name="ident_bf")
+        make_identity(nc, ident_bf[:])
 
         bcol = const.tile([P, NM], F32, name="bcol")
         nc.vector.tensor_scalar(
@@ -90,7 +97,9 @@ def tile_localselfattention_kernel(tc, Q, K, V, mask, out):
             op1=ALU.mult,
         )
         bt = const.tile([P, NM, P], F32, name="bt")
-        nc.vector.tensor_copy(out=bt[:], in_=bcol[:].unsqueeze(2).to_broadcast([P, NM, P]))
+        for mg in range(B * NB):
+            cols = slice(mg * T, (mg + 1) * T)
+            nc.vector.tensor_copy(out=bt[:, cols, :], in_=bcol[:, cols].unsqueeze(2).to_broadcast([P, T, P]))
         keepq = const.tile([P, NM], F32, name="keepq")
         kq_ps = ps_x.tile([P, P], BF16, name="kq_ps", tag="aux")
         nc.tensor.transpose(kq_ps[:], mrow[:], ident_bf[:])
@@ -155,16 +164,16 @@ def tile_localselfattention_kernel(tc, Q, K, V, mask, out):
                     )
             st[("eT_ps", u, h)] = eT_ps
 
-        def pe_pv(u):
+        def pe_pv(u, t0=0, t1=T):
             if not ok(u):
                 return
             ecodes, escales = st[("eq", u)]
             vcodes, vscales = st[("vq", u // VBATCH)]
             cols = slice((u % VBATCH) * D, (u % VBATCH + 1) * D)
-            pv_ps = ps_x.tile([P, T, D], F32, name="pv_ps", tag="aux")
-            for i in range(T):
+            pv_ps = ps_x.tile([P, t1 - t0, D], F32, name="pv_ps", tag="aux")
+            for i in range(t0, t1):
                 nc.tensor.matmul_mx(
-                    out=pv_ps[:, i, :],
+                    out=pv_ps[:, i - t0, :],
                     lhsT=ecodes[:, i * P : (i + 1) * P].bitcast(FP8X4),
                     lhsT_scale=escales[:, i * P : (i + 1) * P],
                     rhs=vcodes[:, cols].bitcast(FP8X4),
@@ -172,7 +181,7 @@ def tile_localselfattention_kernel(tc, Q, K, V, mask, out):
                     start=True,
                     stop=True,
                 )
-            st[("pv_ps", u)] = pv_ps
+            st[("pv_ps", u, t0)] = pv_ps
 
         def gp_copy(out, in0):
             nc.gpsimd.tensor_scalar(out=out, in0=in0, scalar1=1.0, scalar2=0.0, op0=ALU.mult, op1=ALU.add)
@@ -197,7 +206,11 @@ def tile_localselfattention_kernel(tc, Q, K, V, mask, out):
             g, ul = divmod(u, GROUP)
             qki = work.tile([P, T, D, 2], BF16, name="qki", tag="qki")
             gp_copy(qki[:, 0:2, :, :], raw[g][0][:, ul, :, :].rearrange("p (j e) d -> p j d e", e=2))
-            gp_copy(qki[:, 2:4, :, :], raw[g][1][:, ul, :, :].rearrange("p (e w) d -> p w d e", w=2))
+            k_pairs = raw[g][1][:, ul, :, :].rearrange("p (e w) d -> p w d e", w=2)
+            if u == 0:
+                nc.scalar.copy(out=qki[:, 2:4, :, :], in_=k_pairs)
+            else:
+                gp_copy(qki[:, 2:4, :, :], k_pairs)
             st[("qki", u)] = qki
 
         def gp_keep(u):
@@ -234,17 +247,19 @@ def tile_localselfattention_kernel(tc, Q, K, V, mask, out):
             )
             st[("vq", vb)] = (vcodes, vscales)
 
-        def ve_e_quantise(u):
+        def ve_e_quantise(u, t0=0, t1=T):
             if not ok(u):
                 return
-            ecodes = work.tile([P, BS], U32, name="ecodes", tag="ecodes", align_bytes=64)
-            escales = work.tile([P, BS], U8, name="escales", tag="escales", align_bytes=64)
+            if t0 == 0:
+                ecodes = work.tile([P, BS], U32, name="ecodes", tag="ecodes", align_bytes=64)
+                escales = work.tile([P, BS], U8, name="escales", tag="escales", align_bytes=64)
+                st[("eq", u)] = (ecodes, escales)
+            ecodes, escales = st[("eq", u)]
             nc.vector.quantize_mx(
-                out=ecodes[:].bitcast(FP8X4),
-                scales=escales[:],
-                in_=st[("eg", u)][:],
+                out=ecodes[:, t0 * P : t1 * P].bitcast(FP8X4),
+                scales=escales[:, t0 * P : t1 * P],
+                in_=st[("eg", u)][:, t0 * P * T : t1 * P * T],
             )
-            st[("eq", u)] = (ecodes, escales)
 
         def ve_recip(u):
             if not ok(u):
@@ -253,18 +268,18 @@ def tile_localselfattention_kernel(tc, Q, K, V, mask, out):
             nc.vector.reciprocal(out=rinv[:], in_=st[("rsum", u)][:])
             st[("rinv", u)] = rinv
 
-        def ve_out(u):
+        def ve_out(u, t0=0, t1=T):
             if not ok(u):
                 return
-            o_sb = work.tile([P, T, D], F32, name="o_sb", tag="o_sb")
+            o_sb = work.tile([P, t1 - t0, D], F32, name="o_sb", tag="o_sb")
             nc.vector.tensor_tensor(
                 out=o_sb[:],
-                in0=st[("pv_ps", u)][:],
-                in1=st[("rkeep", u)][:].unsqueeze(2).to_broadcast([P, T, D]),
+                in0=st[("pv_ps", u, t0)][:],
+                in1=st[("rkeep", u)][:, t0:t1].unsqueeze(2).to_broadcast([P, t1 - t0, D]),
                 op=ALU.mult,
             )
             nc.sync.dma_start(
-                out=of[u * BS : (u + 1) * BS, :].rearrange("(t p) d -> p t d", p=P), in_=o_sb[:]
+                out=of[u * BS + t0 * P : u * BS + t1 * P, :].rearrange("(t p) d -> p t d", p=P), in_=o_sb[:]
             )
 
         def qk_copy(u, on_vector):
@@ -312,24 +327,30 @@ def tile_localselfattention_kernel(tc, Q, K, V, mask, out):
             u, i = divmod(s, 4)
             pe_scores(u, i)
             if i == 0:
-                pe_pv(u - 4)
+                pe_pv(u - 4, 2 if u - 4 == LAST else 0, T)
             elif i == 1:
                 pe_e_transposes(u - 2, 1)
             elif i == 2:
                 pe_qk_transposes(u + 2)
+                if u - 3 == LAST:
+                    pe_pv(LAST, 0, 2)
             else:
                 pe_e_transposes(u - 1, 0)
             um, im = divmod(s - 2, 4)
             ve_max(um, im)
             if i == 0:
                 qk_copy(u + 1, True)
+                if u - 4 == LAST:
+                    ve_out(LAST, 0, 2)
             elif i == 1:
                 if (u - 2) % VBATCH == 0:
                     ve_v_quantise((u - 2) // VBATCH)
-                ve_e_quantise(u - 3)
+                ve_e_quantise(u - 3, 2 if u - 3 == LAST else 0, T)
                 ve_recip(u - 2)
             elif i == 2:
-                ve_out(u - 4)
+                ve_out(u - 4, 2 if u - 4 == LAST else 0, T)
+            elif u - 2 == LAST:
+                ve_e_quantise(LAST, 0, 2)
             if i == 1:
                 gp_keep(u - 2)
                 gp_qk_pairs(u + 4)

@@ -17,10 +17,9 @@ B, H, S, D, BS = 2, 12, 1024, 128, 512
 NB = S // BS
 UNITS = B * H * NB
 T = BS // P
-GROUP = 1
-VBATCH = 4
-NGROUPS = UNITS // GROUP
+NM = B * NB * T
 LOAD_BUFS = 8
+V_BUFS = 5
 NEG = -10000.0
 NWARM = 6
 LAST = UNITS - 1
@@ -33,14 +32,14 @@ def tile_localselfattention_kernel(tc, Q, K, V, mask, out):
     kf = K.flatten_outer_dims()
     vf = V.flatten_outer_dims()
     of = out.flatten_outer_dims()
-    NM = B * NB * T
 
     with ExitStack() as ctx:
         ctx.enter_context(tc.manual_schedule())
         const = ctx.enter_context(tc.tile_pool(name="const", bufs=1))
         loads = ctx.enter_context(tc.tile_pool(name="loads", bufs=LOAD_BUFS))
-        vpool = ctx.enter_context(tc.tile_pool(name="vpool", bufs=3))
+        vpool = ctx.enter_context(tc.tile_pool(name="vpool", bufs=V_BUFS))
         work = ctx.enter_context(tc.tile_pool(name="work", bufs=3))
+        outs = ctx.enter_context(tc.tile_pool(name="outs", bufs=6))
         stat = ctx.enter_context(tc.tile_pool(name="stat", bufs=8))
         ps_s = ctx.enter_context(tc.psum_pool(name="ps_s", bufs=5))
         ps_x = ctx.enter_context(tc.psum_pool(name="ps_x", bufs=3))
@@ -48,44 +47,49 @@ def tile_localselfattention_kernel(tc, Q, K, V, mask, out):
         raw = {}
         st = {}
 
-        def load_group(g):
-            if g >= NGROUPS:
+        def ok(u):
+            return 0 <= u < UNITS
+
+        def mask_group(u):
+            return (u // (H * NB)) * NB + u % NB
+
+        def load(u):
+            if not ok(u):
                 return
-            rows = slice(g * GROUP * BS, (g + 1) * GROUP * BS)
-            tiles = []
-            for src, tag in ((qf, "q_raw"), (kf, "k_raw"), (vf, "v_raw")):
-                t_raw = loads.tile([P, GROUP, T, D], BF16, name=tag, tag=tag)
-                if tag == "q_raw":
-                    nc.sync.dma_start(
-                        out=t_raw[:].rearrange("x g (h w) d -> x (g h) (w d)", w=2),
-                        in_=src[rows, :].rearrange("(gh x w) d -> x gh (w d)", x=P, w=2),
-                    )
-                else:
-                    nc.sync.dma_start(
-                        out=t_raw[:], in_=src[rows, :].rearrange("(u p t) d -> p u t d", p=P, t=T)
-                    )
-                tiles.append(t_raw)
-            raw[g] = tiles
+            rows = slice(u * BS, (u + 1) * BS)
+            q_raw = loads.tile([P, T, D], BF16, name="q_raw", tag="q_raw")
+            k_raw = loads.tile([P, T, D], BF16, name="k_raw", tag="k_raw")
+            v_raw = loads.tile([P, T, D], BF16, name="v_raw", tag="v_raw")
+            nc.sync.dma_start(
+                out=q_raw[:].rearrange("x (h w) d -> x h (w d)", w=2),
+                in_=qf[rows, :].rearrange("(h x w) d -> x h (w d)", x=P, w=2),
+            )
+            nc.sync.dma_start(out=k_raw[:], in_=kf[rows, :].rearrange("(p t) d -> p t d", t=T))
+            nc.sync.dma_start(out=v_raw[:], in_=vf[rows, :].rearrange("(p t) d -> p t d", t=T))
+            raw[u] = (q_raw, k_raw, v_raw)
 
         mkk = const.tile([P, B, NB * 2, 2], BF16, name="mkk")
         with nc.allow_non_contiguous_dma(reason="the mask, two positions to a piece"):
             nc.scalar.dma_start(out=mkk[:], in_=mask.rearrange("b (nh x w) -> x b nh w", x=P, w=2))
-        load_group(0)
+        load(0)
         warm = const.tile([P, BS], BF16, name="warm")
         nc.vector.memset(warm[:], 0.0)
         for k in range(NWARM):
             w_ps = ps_s.tile([P, BS], F32, name="w_ps", tag="s_ps")
             nc.tensor.matmul(out=w_ps[:], lhsT=warm[:, 0:P], rhs=warm[:], start=True, stop=True)
+        load(1)
         mrow = const.tile([P, P], BF16, name="mrow")
         nc.vector.memset(mrow[:], 0.0)
         nc.sync.dma_start(out=mrow[0:NM, :], in_=mask.rearrange("b (n t p) -> (b n t) p", t=T, p=P))
-        for g in range(1, LOAD_BUFS):
-            load_group(g)
+        for u in range(2, LOAD_BUFS):
+            load(u)
 
         ident_f = const.tile([P, P], F32, name="ident_f")
         make_identity(nc, ident_f[:])
         ident_bf = const.tile([P, P], BF16, name="ident_bf")
         make_identity(nc, ident_bf[:])
+        minus_one = const.tile([P, T], F32, name="minus_one")
+        nc.gpsimd.memset(minus_one[:], -1.0)
 
         bcol = const.tile([P, NM], F32, name="bcol")
         nc.vector.tensor_scalar(
@@ -97,32 +101,35 @@ def tile_localselfattention_kernel(tc, Q, K, V, mask, out):
             op1=ALU.mult,
         )
         bt = const.tile([P, NM, P], F32, name="bt")
-        for mg in range(B * NB):
-            cols = slice(mg * T, (mg + 1) * T)
-            nc.vector.tensor_copy(out=bt[:, cols, :], in_=bcol[:, cols].unsqueeze(2).to_broadcast([P, T, P]))
         keepq = const.tile([P, NM], F32, name="keepq")
-        kq_ps = ps_x.tile([P, P], BF16, name="kq_ps", tag="aux")
-        nc.tensor.transpose(kq_ps[:], mrow[:], ident_bf[:])
-        nc.vector.tensor_single_scalar(out=keepq[:], in_=kq_ps[:, 0:NM], scalar=0.0, op=ALU.not_equal)
 
-        def ok(u):
-            return 0 <= u < UNITS
+        def mask_tile(mg):
+            cols = slice(mg * T, (mg + 1) * T)
+            return bt[:, cols, :], bcol[:, cols].unsqueeze(2).to_broadcast([P, T, P])
 
-        def mask_group(u):
-            return (u // (H * NB)) * NB + u % NB
+        bt_0, bcol_0 = mask_tile(0)
+        nc.vector.tensor_copy(out=bt_0, in_=bcol_0)
+
+        def pe_query_mask():
+            kq_ps = ps_x.tile([P, P], BF16, name="kq_ps", tag="aux")
+            nc.tensor.transpose(kq_ps[:], mrow[:], ident_bf[:])
+            st["kq_ps"] = kq_ps
 
         def pe_qk_transposes(u):
             if not ok(u):
                 return
             qki = st[("qki", u)]
-            qkT_ps = ps_x.tile([P, T, P], F32, name="qkT_ps", tag="aux")
-            for c in range(T):
-                nc.tensor.transpose(
-                    qkT_ps[:, c, :],
-                    qki[:, c, :, :].rearrange("p d e -> p (d e)").bitcast(F32),
-                    ident_f[:],
-                )
-            st[("qkT_ps", u)] = qkT_ps
+            blocks = T // 2 if u == 0 else T
+            st[("qkT_ps", u)] = []
+            for c0 in range(0, T, blocks):
+                qkT_ps = ps_x.tile([P, blocks, P], F32, name="qkT_ps", tag="aux")
+                for c in range(blocks):
+                    nc.tensor.transpose(
+                        qkT_ps[:, c, :],
+                        qki[:, c0 + c, :, :].rearrange("p d e -> p (d e)").bitcast(F32),
+                        ident_f[:],
+                    )
+                st[("qkT_ps", u)].append(qkT_ps)
 
         def pe_scores(u, i):
             if not ok(u):
@@ -149,35 +156,36 @@ def tile_localselfattention_kernel(tc, Q, K, V, mask, out):
             )
             st[("s_ps", u, i)] = s_ps
 
-        def pe_e_transposes(u, h):
+        def pe_e_transposes(u, t0, t1):
             if not ok(u):
                 return
-            e_sb = st[("e_sb", u, h)]
-            eT_ps = ps_x.tile([P, 2, 2, P], F32, name="eT_ps", tag="aux")
-            for ii in range(2):
-                words = e_sb[:, ii, :].bitcast(F32)
+            if u == LAST:
+                eT_ps = ps_s.tile([P, t1 - t0, 2, P], F32, name="eT_ps", tag="s_ps")
+            else:
+                eT_ps = ps_x.tile([P, t1 - t0, 2, P], F32, name="eT_ps", tag="aux")
+            for i in range(t0, t1):
+                words = st[("e_sb", u, i // 2)][:, i % 2, :].bitcast(F32)
                 for w in range(2):
                     nc.tensor.transpose(
-                        eT_ps[:, ii, w, :],
+                        eT_ps[:, i - t0, w, :],
                         words[:, w * P : (w + 1) * P],
                         ident_f[:],
                     )
-            st[("eT_ps", u, h)] = eT_ps
+            st[("eT_ps", u, t0)] = eT_ps
 
         def pe_pv(u, t0=0, t1=T):
             if not ok(u):
                 return
             ecodes, escales = st[("eq", u)]
-            vcodes, vscales = st[("vq", u // VBATCH)]
-            cols = slice((u % VBATCH) * D, (u % VBATCH + 1) * D)
+            vcodes, vscales = st[("vq", u)]
             pv_ps = ps_x.tile([P, t1 - t0, D], F32, name="pv_ps", tag="aux")
             for i in range(t0, t1):
                 nc.tensor.matmul_mx(
                     out=pv_ps[:, i - t0, :],
                     lhsT=ecodes[:, i * P : (i + 1) * P].bitcast(FP8X4),
                     lhsT_scale=escales[:, i * P : (i + 1) * P],
-                    rhs=vcodes[:, cols].bitcast(FP8X4),
-                    rhs_scale=vscales[:, cols],
+                    rhs=vcodes[:].bitcast(FP8X4),
+                    rhs_scale=vscales[:],
                     start=True,
                     stop=True,
                 )
@@ -189,27 +197,25 @@ def tile_localselfattention_kernel(tc, Q, K, V, mask, out):
         def gp_v_regroup(u):
             if not ok(u):
                 return
-            g, ul = divmod(u, GROUP)
-            vb, vl = divmod(u, VBATCH)
-            if vl == 0:
-                st[("vg", vb)] = vpool.tile(
-                    [P, VBATCH, D, T], BF16, name="vg", tag="vg", align_bytes=64
-                )
+            st[("vg", u)] = vpool.tile([P, D, T], BF16, name="vg", tag="vg", align_bytes=64)
             gp_copy(
-                st[("vg", vb)][:, vl, :, :].rearrange("p d (w e) -> p d w e", e=2),
-                raw[g][2][:, ul, :, :].rearrange("p (e w) d -> p d w e", w=2),
+                st[("vg", u)][:].rearrange("p d (w e) -> p d w e", e=2),
+                raw[u][2][:].rearrange("p (e w) d -> p d w e", w=2),
             )
 
         def gp_qk_pairs(u):
             if not ok(u):
                 return
-            g, ul = divmod(u, GROUP)
             qki = work.tile([P, T, D, 2], BF16, name="qki", tag="qki")
-            gp_copy(qki[:, 0:2, :, :], raw[g][0][:, ul, :, :].rearrange("p (j e) d -> p j d e", e=2))
-            k_pairs = raw[g][1][:, ul, :, :].rearrange("p (e w) d -> p w d e", w=2)
+            q_pairs = raw[u][0][:].rearrange("p (j e) d -> p j d e", e=2)
+            k_pairs = raw[u][1][:].rearrange("p (e w) d -> p w d e", w=2)
             if u == 0:
+                nc.vector.tensor_copy(out=qki[:, 0:2, :, :], in_=q_pairs)
                 nc.scalar.copy(out=qki[:, 2:4, :, :], in_=k_pairs)
+                bt_1, bcol_1 = mask_tile(1)
+                nc.scalar.copy(out=bt_1, in_=bcol_1)
             else:
+                gp_copy(qki[:, 0:2, :, :], q_pairs)
                 gp_copy(qki[:, 2:4, :, :], k_pairs)
             st[("qki", u)] = qki
 
@@ -217,14 +223,16 @@ def tile_localselfattention_kernel(tc, Q, K, V, mask, out):
             if not ok(u):
                 return
             mg = mask_group(u)
+            rinv = stat.tile([P, T], F32, name="rinv", tag="rinv")
+            nc.gpsimd.tensor_tensor(out=rinv[:], in0=st[("rsum", u)][:], in1=minus_one[:], op=ALU.pow)
             rkeep = stat.tile([P, T], F32, name="rkeep", tag="rkeep")
             nc.gpsimd.tensor_tensor(
-                out=rkeep[:],
-                in0=st[("rinv", u)][:],
-                in1=keepq[:, mg * T : (mg + 1) * T],
-                op=ALU.mult,
+                out=rkeep[:], in0=rinv[:], in1=keepq[:, mg * T : (mg + 1) * T], op=ALU.mult
             )
             st[("rkeep", u)] = rkeep
+
+        def ve_query_mask():
+            nc.vector.tensor_single_scalar(out=keepq[:], in_=st["kq_ps"][:, 0:NM], scalar=0.0, op=ALU.not_equal)
 
         def ve_max(u, i):
             if not ok(u):
@@ -235,17 +243,17 @@ def tile_localselfattention_kernel(tc, Q, K, V, mask, out):
             )
             st[("negm", u, i)] = negm
 
-        def ve_v_quantise(vb):
-            if not 0 <= vb < UNITS // VBATCH:
+        def ve_v_quantise(u):
+            if not ok(u):
                 return
-            vcodes = vpool.tile([P, VBATCH * D], U32, name="vcodes", tag="vcodes", align_bytes=64)
-            vscales = vpool.tile([P, VBATCH * D], U8, name="vscales", tag="vscales", align_bytes=64)
+            vcodes = vpool.tile([P, D], U32, name="vcodes", tag="vcodes", align_bytes=64)
+            vscales = vpool.tile([P, D], U8, name="vscales", tag="vscales", align_bytes=64)
             nc.vector.quantize_mx(
                 out=vcodes[:].bitcast(FP8X4),
                 scales=vscales[:],
-                in_=st[("vg", vb)][:].rearrange("p u d j -> p (u d j)"),
+                in_=st[("vg", u)][:].rearrange("p d j -> p (d j)"),
             )
-            st[("vq", vb)] = (vcodes, vscales)
+            st[("vq", u)] = (vcodes, vscales)
 
         def ve_e_quantise(u, t0=0, t1=T):
             if not ok(u):
@@ -261,17 +269,10 @@ def tile_localselfattention_kernel(tc, Q, K, V, mask, out):
                 in_=st[("eg", u)][:, t0 * P * T : t1 * P * T],
             )
 
-        def ve_recip(u):
-            if not ok(u):
-                return
-            rinv = stat.tile([P, T], F32, name="rinv", tag="rinv")
-            nc.vector.reciprocal(out=rinv[:], in_=st[("rsum", u)][:])
-            st[("rinv", u)] = rinv
-
         def ve_out(u, t0=0, t1=T):
             if not ok(u):
                 return
-            o_sb = work.tile([P, t1 - t0, D], F32, name="o_sb", tag="o_sb")
+            o_sb = outs.tile([P, t1 - t0, D], F32, name="o_sb", tag="o_sb")
             nc.vector.tensor_tensor(
                 out=o_sb[:],
                 in0=st[("pv_ps", u, t0)][:],
@@ -283,15 +284,22 @@ def tile_localselfattention_kernel(tc, Q, K, V, mask, out):
             )
 
         def qk_copy(u, on_vector):
-            if not ok(u) or (u % 2 == 1) != on_vector:
+            if not ok(u) or (u > 0 and (u % 2 == 1) != on_vector):
                 return
-            qkT = work.tile([P, 2 * BS], BF16, name="qkT", tag="qkT")
-            words = st[("qkT_ps", u)][:].rearrange("p c x -> p (c x)")
-            if on_vector:
-                nc.vector.tensor_copy(out=qkT[:].bitcast(F32), in_=words)
+            if ("qkT", u) not in st:
+                st[("qkT", u)] = work.tile([P, 2 * BS], BF16, name="qkT", tag="qkT")
+            qkT_words = st[("qkT", u)][:].bitcast(F32)
+            banks = st[("qkT_ps", u)]
+            if u == 0:
+                bank = banks[0] if on_vector else banks[1]
+                qkT_words = qkT_words[:, 0 : BS // 2] if on_vector else qkT_words[:, BS // 2 : BS]
             else:
-                nc.scalar.copy(out=qkT[:].bitcast(F32), in_=words)
-            st[("qkT", u)] = qkT
+                bank = banks[0]
+            words = bank[:].rearrange("p c x -> p (c x)")
+            if on_vector:
+                nc.vector.tensor_copy(out=qkT_words, in_=words)
+            else:
+                nc.scalar.copy(out=qkT_words, in_=words)
 
         def se_exp(u, i):
             if not ok(u):
@@ -310,58 +318,94 @@ def tile_localselfattention_kernel(tc, Q, K, V, mask, out):
                 accum_out=st[("rsum", u)][:, i : i + 1],
             )
 
-        def se_e_copy(u, h):
+        def se_e_copy(u, t0, t1):
             if not ok(u):
                 return
-            if h == 0:
+            if t0 == 0:
                 st[("eg", u)] = work.tile([P, T * P * T], BF16, name="eg", tag="eg", align_bytes=64)
-            half = T * P * T // 2
             nc.scalar.copy(
-                out=st[("eg", u)][:, h * half : (h + 1) * half]
+                out=st[("eg", u)][:, t0 * P * T : t1 * P * T]
                 .bitcast(F32)
-                .rearrange("p (i q w) -> p i q w", i=2, w=2),
-                in_=st[("eT_ps", u, h)][:].rearrange("p i w q -> p i q w"),
+                .rearrange("p (i q w) -> p i q w", i=t1 - t0, w=2),
+                in_=st[("eT_ps", u, t0)][:].rearrange("p i w q -> p i q w"),
             )
 
         for s in range(-20, 4 * UNITS + 20):
             u, i = divmod(s, 4)
             pe_scores(u, i)
+            if s == 0:
+                pe_qk_transposes(1)
+            if s == 2:
+                pe_query_mask()
             if i == 0:
-                pe_pv(u - 4, 2 if u - 4 == LAST else 0, T)
+                if u - 4 != LAST:
+                    pe_pv(u - 4)
             elif i == 1:
-                pe_e_transposes(u - 2, 1)
+                if u - 2 != LAST:
+                    pe_e_transposes(u - 2, 2, 4)
             elif i == 2:
-                pe_qk_transposes(u + 2)
-                if u - 3 == LAST:
-                    pe_pv(LAST, 0, 2)
+                if u + 2 != 1:
+                    pe_qk_transposes(u + 2)
             else:
-                pe_e_transposes(u - 1, 0)
+                if u - 1 != LAST:
+                    pe_e_transposes(u - 1, 0, 2)
+            tl = s - 6 - 4 * LAST
+            if 0 <= tl < T:
+                pe_e_transposes(LAST, tl, tl + 1)
+            if s == 4 * LAST + 15:
+                for t0 in range(0, T, 2):
+                    pe_pv(LAST, t0, t0 + 2)
             um, im = divmod(s - 2, 4)
             ve_max(um, im)
+            if s == 2:
+                qk_copy(1, True)
+            if s == 4:
+                ve_query_mask()
             if i == 0:
-                qk_copy(u + 1, True)
-                if u - 4 == LAST:
-                    ve_out(LAST, 0, 2)
+                if s != 0:
+                    qk_copy(u + 1, True)
             elif i == 1:
-                if (u - 2) % VBATCH == 0:
-                    ve_v_quantise((u - 2) // VBATCH)
-                ve_e_quantise(u - 3, 2 if u - 3 == LAST else 0, T)
-                ve_recip(u - 2)
+                if u - 3 != LAST:
+                    ve_e_quantise(u - 3)
+                if u - 3 < LAST - 2:
+                    ve_v_quantise(u - 3)
+                elif u - 3 == LAST - 2:
+                    for v in range(LAST - 2, UNITS):
+                        ve_v_quantise(v)
             elif i == 2:
-                ve_out(u - 4, 2 if u - 4 == LAST else 0, T)
-            elif u - 2 == LAST:
-                ve_e_quantise(LAST, 0, 2)
+                if u - 4 != LAST:
+                    ve_out(u - 4)
+            tl = s - 10 - 4 * LAST
+            if 0 <= tl < T:
+                ve_e_quantise(LAST, tl, tl + 1)
+            if s == 4 * LAST + 17:
+                for t0 in range(0, T, 2):
+                    ve_out(LAST, t0, t0 + 2)
             if i == 1:
+                if u + 2 < V_BUFS:
+                    gp_qk_pairs(u + 4)
+                    gp_v_regroup(u + 2)
+                else:
+                    gp_v_regroup(u + 2)
+                    gp_qk_pairs(u + 4)
                 gp_keep(u - 2)
-                gp_qk_pairs(u + 4)
-                gp_v_regroup(u + 2)
-                if ok(u + 2) and (u + 2) % GROUP == GROUP - 1:
-                    load_group((u + 2) // GROUP + LOAD_BUFS)
+                if H - B * NB + 2 <= u < H:
+                    bt_u, bcol_u = mask_tile(u - H + B * NB)
+                    gp_copy(bt_u, bcol_u)
+                if ok(u + 2):
+                    load(u + 2 + LOAD_BUFS)
+            if s == 4 * LAST + 7:
+                se_e_copy(LAST - 1, 2, 4)
             ux, ix = divmod(s - 4, 4)
             se_exp(ux, ix)
             if i == 0:
                 qk_copy(u + 1, False)
             elif i == 1:
-                se_e_copy(u - 2, 0)
+                if u - 2 != LAST:
+                    se_e_copy(u - 2, 0, 2)
             elif i == 3:
-                se_e_copy(u - 2, 1)
+                if u - 2 < LAST - 1:
+                    se_e_copy(u - 2, 2, 4)
+            tl = s - 8 - 4 * LAST
+            if 0 <= tl < T:
+                se_e_copy(LAST, tl, tl + 1)

@@ -88,8 +88,6 @@ def tile_localselfattention_kernel(tc, Q, K, V, mask, out):
         make_identity(nc, ident_f[:])
         ident_bf = const.tile([P, P], BF16, name="ident_bf")
         make_identity(nc, ident_bf[:])
-        minus_one = const.tile([P, T], F32, name="minus_one")
-        nc.gpsimd.memset(minus_one[:], -1.0)
 
         bcol = const.tile([P, NM], F32, name="bcol")
         nc.vector.tensor_scalar(
@@ -223,13 +221,15 @@ def tile_localselfattention_kernel(tc, Q, K, V, mask, out):
             if not ok(u):
                 return
             mg = mask_group(u)
-            rinv = stat.tile([P, T], F32, name="rinv", tag="rinv")
-            nc.gpsimd.tensor_tensor(out=rinv[:], in0=st[("rsum", u)][:], in1=minus_one[:], op=ALU.pow)
-            rkeep = stat.tile([P, T], F32, name="rkeep", tag="rkeep")
+            rkeep = stat.tile([P, NB * T], F32, name="rkeep", tag="rkeep")
             nc.gpsimd.tensor_tensor(
-                out=rkeep[:], in0=rinv[:], in1=keepq[:, mg * T : (mg + 1) * T], op=ALU.mult
+                out=rkeep[:],
+                in0=st[("rinv", u)][:],
+                in1=keepq[:, mg * T : (mg + NB) * T],
+                op=ALU.mult,
             )
-            st[("rkeep", u)] = rkeep
+            for n in range(NB):
+                st[("rkeep", u + n)] = rkeep[:, n * T : (n + 1) * T]
 
         def ve_query_mask():
             nc.vector.tensor_single_scalar(out=keepq[:], in_=st["kq_ps"][:, 0:NM], scalar=0.0, op=ALU.not_equal)
@@ -269,6 +269,13 @@ def tile_localselfattention_kernel(tc, Q, K, V, mask, out):
                 in_=st[("eg", u)][:, t0 * P * T : t1 * P * T],
             )
 
+        def ve_recip(u):
+            if not ok(u):
+                return
+            rinv = stat.tile([P, NB * T], F32, name="rinv", tag="rinv")
+            nc.vector.reciprocal(out=rinv[:], in_=st[("rsum", u)][:])
+            st[("rinv", u)] = rinv
+
         def ve_out(u, t0=0, t1=T):
             if not ok(u):
                 return
@@ -305,8 +312,9 @@ def tile_localselfattention_kernel(tc, Q, K, V, mask, out):
             if not ok(u):
                 return
             h, ii = divmod(i, 2)
-            if i == 0:
-                st[("rsum", u)] = stat.tile([P, T], F32, name="rsum", tag="rsum")
+            pair, n = divmod(u, NB)
+            if n == 0 and i == 0:
+                st[("rsum", u)] = stat.tile([P, NB * T], F32, name="rsum", tag="rsum")
             if ii == 0:
                 st[("e_sb", u, h)] = work.tile([P, 2, BS], BF16, name="e_sb", tag="e_sb")
             nc.scalar.activation(
@@ -315,7 +323,7 @@ def tile_localselfattention_kernel(tc, Q, K, V, mask, out):
                 func=ACT.Exp,
                 bias=st[("negm", u, i)][:],
                 scale=1.0,
-                accum_out=st[("rsum", u)][:, i : i + 1],
+                accum_out=st[("rsum", pair * NB)][:, n * T + i : n * T + i + 1],
             )
 
         def se_e_copy(u, t0, t1):
@@ -367,6 +375,8 @@ def tile_localselfattention_kernel(tc, Q, K, V, mask, out):
             elif i == 1:
                 if u - 3 != LAST:
                     ve_e_quantise(u - 3)
+                if u % NB == 1:
+                    ve_recip(u - 3)
                 if u - 3 < LAST - 2:
                     ve_v_quantise(u - 3)
                 elif u - 3 == LAST - 2:
@@ -387,8 +397,10 @@ def tile_localselfattention_kernel(tc, Q, K, V, mask, out):
                     gp_v_regroup(u + 2)
                 else:
                     gp_v_regroup(u + 2)
+                if u % NB == 1:
+                    gp_keep(u - 3)
+                if u + 2 >= V_BUFS:
                     gp_qk_pairs(u + 4)
-                gp_keep(u - 2)
                 if H - B * NB + 2 <= u < H:
                     bt_u, bcol_u = mask_tile(u - H + B * NB)
                     gp_copy(bt_u, bcol_u)

@@ -20,6 +20,7 @@ T = BS // P
 NM = B * NB * T
 LOAD_BUFS = 8
 V_BUFS = 5
+DIRECT = 2
 NEG = -10000.0
 NWARM = 6
 LAST = UNITS - 1
@@ -45,6 +46,7 @@ def tile_localselfattention_kernel(tc, Q, K, V, mask, out):
         ps_x = ctx.enter_context(tc.psum_pool(name="ps_x", bufs=3))
 
         raw = {}
+        raw_v = {}
         st = {}
 
         def ok(u):
@@ -53,41 +55,57 @@ def tile_localselfattention_kernel(tc, Q, K, V, mask, out):
         def mask_group(u):
             return (u // (H * NB)) * NB + u % NB
 
-        def load(u):
+        def load_qk(u):
             if not ok(u):
                 return
             rows = slice(u * BS, (u + 1) * BS)
             q_raw = loads.tile([P, T, D], BF16, name="q_raw", tag="q_raw")
             k_raw = loads.tile([P, T, D], BF16, name="k_raw", tag="k_raw")
+            in_runs = "(h x w) d -> x h (w d)"
+            out_runs = "x (h w) d -> x h (w d)"
+            if u < DIRECT:
+                nc.sync.dma_start(out=q_raw[:], in_=qf[rows, :].rearrange("(t p) d -> p t d", p=P))
+                nc.sync.dma_start(
+                    out=k_raw[:].rearrange(out_runs, w=2), in_=kf[rows, :].rearrange(in_runs, x=P, w=2)
+                )
+            else:
+                nc.sync.dma_start(
+                    out=q_raw[:].rearrange(out_runs, w=2), in_=qf[rows, :].rearrange(in_runs, x=P, w=2)
+                )
+                nc.sync.dma_start(out=k_raw[:], in_=kf[rows, :].rearrange("(p t) d -> p t d", t=T))
+            raw[u] = (q_raw, k_raw)
+
+        def load_v(u):
+            if not ok(u):
+                return
             v_raw = loads.tile([P, T, D], BF16, name="v_raw", tag="v_raw")
             nc.sync.dma_start(
-                out=q_raw[:].rearrange("x (h w) d -> x h (w d)", w=2),
-                in_=qf[rows, :].rearrange("(h x w) d -> x h (w d)", x=P, w=2),
+                out=v_raw[:], in_=vf[u * BS : (u + 1) * BS, :].rearrange("(p t) d -> p t d", t=T)
             )
-            nc.sync.dma_start(out=k_raw[:], in_=kf[rows, :].rearrange("(p t) d -> p t d", t=T))
-            nc.sync.dma_start(out=v_raw[:], in_=vf[rows, :].rearrange("(p t) d -> p t d", t=T))
-            raw[u] = (q_raw, k_raw, v_raw)
+            raw_v[u] = v_raw
 
         mkk = const.tile([P, B, NB * 2, 2], BF16, name="mkk")
         with nc.allow_non_contiguous_dma(reason="the mask, two positions to a piece"):
             nc.scalar.dma_start(out=mkk[:], in_=mask.rearrange("b (nh x w) -> x b nh w", x=P, w=2))
-        load(0)
+        for u in range(DIRECT + 1):
+            load_qk(u)
         warm = const.tile([P, BS], BF16, name="warm")
         nc.vector.memset(warm[:], 0.0)
         for k in range(NWARM):
             w_ps = ps_s.tile([P, BS], F32, name="w_ps", tag="s_ps")
             nc.tensor.matmul(out=w_ps[:], lhsT=warm[:, 0:P], rhs=warm[:], start=True, stop=True)
-        load(1)
         mrow = const.tile([P, P], BF16, name="mrow")
         nc.vector.memset(mrow[:], 0.0)
         nc.sync.dma_start(out=mrow[0:NM, :], in_=mask.rearrange("b (n t p) -> (b n t) p", t=T, p=P))
-        for u in range(2, LOAD_BUFS):
-            load(u)
+        for u in range(LOAD_BUFS):
+            load_v(u)
+            if DIRECT + 1 + u < LOAD_BUFS:
+                load_qk(DIRECT + 1 + u)
 
-        ident_f = const.tile([P, P], F32, name="ident_f")
-        make_identity(nc, ident_f[:])
         ident_bf = const.tile([P, P], BF16, name="ident_bf")
         make_identity(nc, ident_bf[:])
+        ident_f = const.tile([P, P], F32, name="ident_f")
+        make_identity(nc, ident_f[:])
 
         bcol = const.tile([P, NM], F32, name="bcol")
         nc.vector.tensor_scalar(
@@ -113,21 +131,25 @@ def tile_localselfattention_kernel(tc, Q, K, V, mask, out):
             nc.tensor.transpose(kq_ps[:], mrow[:], ident_bf[:])
             st["kq_ps"] = kq_ps
 
+        def pe_direct_transposes(u):
+            for x, order in ((0, (0, 1, 2, 3)), (1, (0, 2, 1, 3))):
+                xT_ps = ps_x.tile([P, T, P], BF16, name="xT_ps", tag="aux")
+                for c in range(T):
+                    nc.tensor.transpose(xT_ps[:, c, :], raw[u][x][:, order[c], :], ident_bf[:])
+                st[("xT_ps", u, x)] = xT_ps
+
         def pe_qk_transposes(u):
-            if not ok(u):
+            if not DIRECT <= u < UNITS:
                 return
             qki = st[("qki", u)]
-            blocks = T // 2 if u == 0 else T
-            st[("qkT_ps", u)] = []
-            for c0 in range(0, T, blocks):
-                qkT_ps = ps_x.tile([P, blocks, P], F32, name="qkT_ps", tag="aux")
-                for c in range(blocks):
-                    nc.tensor.transpose(
-                        qkT_ps[:, c, :],
-                        qki[:, c0 + c, :, :].rearrange("p d e -> p (d e)").bitcast(F32),
-                        ident_f[:],
-                    )
-                st[("qkT_ps", u)].append(qkT_ps)
+            qkT_ps = ps_x.tile([P, T, P], F32, name="qkT_ps", tag="aux")
+            for c in range(T):
+                nc.tensor.transpose(
+                    qkT_ps[:, c, :],
+                    qki[:, c, :, :].rearrange("p d e -> p (d e)").bitcast(F32),
+                    ident_f[:],
+                )
+            st[("qkT_ps", u)] = qkT_ps
 
         def pe_scores(u, i):
             if not ok(u):
@@ -198,23 +220,15 @@ def tile_localselfattention_kernel(tc, Q, K, V, mask, out):
             st[("vg", u)] = vpool.tile([P, D, T], BF16, name="vg", tag="vg", align_bytes=64)
             gp_copy(
                 st[("vg", u)][:].rearrange("p d (w e) -> p d w e", e=2),
-                raw[u][2][:].rearrange("p (e w) d -> p d w e", w=2),
+                raw_v[u][:].rearrange("p (e w) d -> p d w e", w=2),
             )
 
         def gp_qk_pairs(u):
-            if not ok(u):
+            if not DIRECT <= u < UNITS:
                 return
             qki = work.tile([P, T, D, 2], BF16, name="qki", tag="qki")
-            q_pairs = raw[u][0][:].rearrange("p (j e) d -> p j d e", e=2)
-            k_pairs = raw[u][1][:].rearrange("p (e w) d -> p w d e", w=2)
-            if u == 0:
-                nc.vector.tensor_copy(out=qki[:, 0:2, :, :], in_=q_pairs)
-                nc.scalar.copy(out=qki[:, 2:4, :, :], in_=k_pairs)
-                bt_1, bcol_1 = mask_tile(1)
-                nc.scalar.copy(out=bt_1, in_=bcol_1)
-            else:
-                gp_copy(qki[:, 0:2, :, :], q_pairs)
-                gp_copy(qki[:, 2:4, :, :], k_pairs)
+            gp_copy(qki[:, 0:2, :, :], raw[u][0][:].rearrange("p (j e) d -> p j d e", e=2))
+            gp_copy(qki[:, 2:4, :, :], raw[u][1][:].rearrange("p (e w) d -> p w d e", w=2))
             st[("qki", u)] = qki
 
         def gp_keep(u):
@@ -290,23 +304,24 @@ def tile_localselfattention_kernel(tc, Q, K, V, mask, out):
                 out=of[u * BS + t0 * P : u * BS + t1 * P, :].rearrange("(t p) d -> p t d", p=P), in_=o_sb[:]
             )
 
-        def qk_copy(u, on_vector):
-            if not ok(u) or (u > 0 and (u % 2 == 1) != on_vector):
-                return
-            if ("qkT", u) not in st:
+        def direct_copy(u, x, engine_copy):
+            if x == 0:
                 st[("qkT", u)] = work.tile([P, 2 * BS], BF16, name="qkT", tag="qkT")
-            qkT_words = st[("qkT", u)][:].bitcast(F32)
-            banks = st[("qkT_ps", u)]
-            if u == 0:
-                bank = banks[0] if on_vector else banks[1]
-                qkT_words = qkT_words[:, 0 : BS // 2] if on_vector else qkT_words[:, BS // 2 : BS]
-            else:
-                bank = banks[0]
-            words = bank[:].rearrange("p c x -> p (c x)")
+            engine_copy(
+                out=st[("qkT", u)][:, x * BS : (x + 1) * BS],
+                in_=st[("xT_ps", u, x)][:].rearrange("p c x -> p (c x)"),
+            )
+
+        def qk_copy(u, on_vector):
+            if not DIRECT <= u < UNITS or (u % 2 == 0) != on_vector:
+                return
+            qkT = work.tile([P, 2 * BS], BF16, name="qkT", tag="qkT")
+            words = st[("qkT_ps", u)][:].rearrange("p c x -> p (c x)")
             if on_vector:
-                nc.vector.tensor_copy(out=qkT_words, in_=words)
+                nc.vector.tensor_copy(out=qkT[:].bitcast(F32), in_=words)
             else:
-                nc.scalar.copy(out=qkT_words, in_=words)
+                nc.scalar.copy(out=qkT[:].bitcast(F32), in_=words)
+            st[("qkT", u)] = qkT
 
         def se_exp(u, i):
             if not ok(u):
@@ -338,12 +353,17 @@ def tile_localselfattention_kernel(tc, Q, K, V, mask, out):
                 in_=st[("eT_ps", u, t0)][:].rearrange("p i w q -> p i q w"),
             )
 
+        pe_direct_transposes(0)
+        direct_copy(0, 0, nc.vector.tensor_copy)
+        direct_copy(0, 1, nc.scalar.copy)
+        bt_1, bcol_1 = mask_tile(1)
+        nc.scalar.copy(out=bt_1, in_=bcol_1)
         for s in range(-20, 4 * UNITS + 20):
             u, i = divmod(s, 4)
             pe_scores(u, i)
-            if s == 0:
-                pe_qk_transposes(1)
-            if s == 2:
+            if s == 1:
+                pe_direct_transposes(1)
+            if s == 5:
                 pe_query_mask()
             if i == 0:
                 if u - 4 != LAST:
@@ -352,8 +372,7 @@ def tile_localselfattention_kernel(tc, Q, K, V, mask, out):
                 if u - 2 != LAST:
                     pe_e_transposes(u - 2, 2, 4)
             elif i == 2:
-                if u + 2 != 1:
-                    pe_qk_transposes(u + 2)
+                pe_qk_transposes(u + 2)
             else:
                 if u - 1 != LAST:
                     pe_e_transposes(u - 1, 0, 2)
@@ -365,13 +384,13 @@ def tile_localselfattention_kernel(tc, Q, K, V, mask, out):
                     pe_pv(LAST, t0, t0 + 2)
             um, im = divmod(s - 2, 4)
             ve_max(um, im)
-            if s == 2:
-                qk_copy(1, True)
-            if s == 4:
+            if s == 3:
+                for x in range(2):
+                    direct_copy(1, x, nc.vector.tensor_copy)
+            if s == 7:
                 ve_query_mask()
             if i == 0:
-                if s != 0:
-                    qk_copy(u + 1, True)
+                qk_copy(u + 1, True)
             elif i == 1:
                 if u - 3 != LAST:
                     ve_e_quantise(u - 3)
@@ -404,8 +423,9 @@ def tile_localselfattention_kernel(tc, Q, K, V, mask, out):
                 if H - B * NB + 2 <= u < H:
                     bt_u, bcol_u = mask_tile(u - H + B * NB)
                     gp_copy(bt_u, bcol_u)
-                if ok(u + 2):
-                    load(u + 2 + LOAD_BUFS)
+                if ok(u):
+                    load_qk(u + LOAD_BUFS)
+                    load_v(u + LOAD_BUFS)
             if s == 4 * LAST + 7:
                 se_e_copy(LAST - 1, 2, 4)
             ux, ix = divmod(s - 4, 4)

@@ -22,7 +22,7 @@ LOAD_BUFS = 8
 V_BUFS = 5
 DIRECT = 2
 NEG = -10000.0
-NWARM = 6
+NWARM = 5
 LAST = UNITS - 1
 FLOPS = 2 * 2 * BS * BS * D * UNITS
 
@@ -63,15 +63,14 @@ def tile_localselfattention_kernel(tc, Q, K, V, mask, out):
             k_raw = loads.tile([P, T, D], BF16, name="k_raw", tag="k_raw")
             in_runs = "(h x w) d -> x h (w d)"
             out_runs = "x (h w) d -> x h (w d)"
+            nc.sync.dma_start(
+                out=q_raw[:].rearrange(out_runs, w=2), in_=qf[rows, :].rearrange(in_runs, x=P, w=2)
+            )
             if u < DIRECT:
-                nc.sync.dma_start(out=q_raw[:], in_=qf[rows, :].rearrange("(t p) d -> p t d", p=P))
                 nc.sync.dma_start(
                     out=k_raw[:].rearrange(out_runs, w=2), in_=kf[rows, :].rearrange(in_runs, x=P, w=2)
                 )
             else:
-                nc.sync.dma_start(
-                    out=q_raw[:].rearrange(out_runs, w=2), in_=qf[rows, :].rearrange(in_runs, x=P, w=2)
-                )
                 nc.sync.dma_start(out=k_raw[:], in_=kf[rows, :].rearrange("(p t) d -> p t d", t=T))
             raw[u] = (q_raw, k_raw)
 
@@ -84,9 +83,9 @@ def tile_localselfattention_kernel(tc, Q, K, V, mask, out):
             )
             raw_v[u] = v_raw
 
-        mkk = const.tile([P, B, NB * 2, 2], BF16, name="mkk")
-        with nc.allow_non_contiguous_dma(reason="the mask, two positions to a piece"):
-            nc.scalar.dma_start(out=mkk[:], in_=mask.rearrange("b (nh x w) -> x b nh w", x=P, w=2))
+        mrow = const.tile([P, BS], BF16, name="mrow")
+        nc.vector.memset(mrow[:], 0.0)
+        nc.scalar.dma_start(out=mrow[0 : B * NB, :], in_=mask.rearrange("b (n k) -> (b n) k", k=BS))
         for u in range(DIRECT + 1):
             load_qk(u)
         warm = const.tile([P, BS], BF16, name="warm")
@@ -94,9 +93,6 @@ def tile_localselfattention_kernel(tc, Q, K, V, mask, out):
         for k in range(NWARM):
             w_ps = ps_s.tile([P, BS], F32, name="w_ps", tag="s_ps")
             nc.tensor.matmul(out=w_ps[:], lhsT=warm[:, 0:P], rhs=warm[:], start=True, stop=True)
-        mrow = const.tile([P, P], BF16, name="mrow")
-        nc.vector.memset(mrow[:], 0.0)
-        nc.sync.dma_start(out=mrow[0:NM, :], in_=mask.rearrange("b (n t p) -> (b n t) p", t=T, p=P))
         for u in range(LOAD_BUFS):
             load_v(u)
             if DIRECT + 1 + u < LOAD_BUFS:
@@ -107,36 +103,26 @@ def tile_localselfattention_kernel(tc, Q, K, V, mask, out):
         ident_f = const.tile([P, P], F32, name="ident_f")
         make_identity(nc, ident_f[:])
 
-        bcol = const.tile([P, NM], F32, name="bcol")
-        nc.vector.tensor_scalar(
-            out=bcol[:],
-            in0=mkk[:].rearrange("p b a w -> p (b a w)"),
-            scalar1=0.0,
-            scalar2=NEG,
-            op0=ALU.is_equal,
-            op1=ALU.mult,
-        )
         bt = const.tile([P, NM, P], F32, name="bt")
-        keepq = const.tile([P, NM], F32, name="keepq")
+        keep_direct = const.tile([P, B * NB, T], F32, name="keep_direct")
+        keepq = const.tile([P, B * NB, T], F32, name="keepq")
 
         def mask_tile(mg):
-            cols = slice(mg * T, (mg + 1) * T)
-            return bt[:, cols, :], bcol[:, cols].unsqueeze(2).to_broadcast([P, T, P])
+            return bt[:, mg * T : (mg + 1) * T, :], bcol[:, mg, :].unsqueeze(2).to_broadcast([P, T, P])
 
-        bt_0, bcol_0 = mask_tile(0)
-        nc.vector.tensor_copy(out=bt_0, in_=bcol_0)
 
         def pe_query_mask():
-            kq_ps = ps_x.tile([P, P], BF16, name="kq_ps", tag="aux")
-            nc.tensor.transpose(kq_ps[:], mrow[:], ident_bf[:])
-            st["kq_ps"] = kq_ps
+            tiles_ps = ps_x.tile([P, T, P], BF16, name="tiles_ps", tag="aux")
+            for t in range(T):
+                nc.tensor.transpose(tiles_ps[:, t, :], mrow[:, t * P : (t + 1) * P], ident_bf[:])
+            st["tiles_ps"] = tiles_ps
 
-        def pe_direct_transposes(u):
-            for x, order in ((0, (0, 1, 2, 3)), (1, (0, 2, 1, 3))):
-                xT_ps = ps_x.tile([P, T, P], BF16, name="xT_ps", tag="aux")
-                for c in range(T):
-                    nc.tensor.transpose(xT_ps[:, c, :], raw[u][x][:, order[c], :], ident_bf[:])
-                st[("xT_ps", u, x)] = xT_ps
+        def pe_direct_transposes(u, x):
+            order = ((0, 1, 2, 3), (0, 2, 1, 3))[x]
+            xT_ps = ps_x.tile([P, T, P], BF16, name="xT_ps", tag="aux")
+            for c in range(T):
+                nc.tensor.transpose(xT_ps[:, c, :], raw[u][x][:, order[c], :], ident_bf[:])
+            st[("xT_ps", u, x)] = xT_ps
 
         def pe_qk_transposes(u):
             if not DIRECT <= u < UNITS:
@@ -159,9 +145,14 @@ def tile_localselfattention_kernel(tc, Q, K, V, mask, out):
             s_ps = ps_s.tile([P, BS], F32, name="s_ps", tag="s_ps")
             for t in range(T):
                 w, h = divmod(t, 2)
+                c = 2 * h + w
+                if u == 0:
+                    bias = bcol[:, mg, c : c + 1].to_broadcast([P, P])
+                else:
+                    bias = bt[:, mg * T + c, :]
                 nc.tensor.matmul(
                     out=s_ps[:, t * P : (t + 1) * P],
-                    lhsT=bt[:, mg * T + 2 * h + w, :],
+                    lhsT=bias,
                     rhs=ident_f[:],
                     is_transpose=True,
                     start=(t == 0),
@@ -235,18 +226,24 @@ def tile_localselfattention_kernel(tc, Q, K, V, mask, out):
             if not ok(u):
                 return
             mg = mask_group(u)
+            keep = keep_direct if u < DIRECT else keepq
             rkeep = stat.tile([P, NB * T], F32, name="rkeep", tag="rkeep")
             nc.gpsimd.tensor_tensor(
                 out=rkeep[:],
                 in0=st[("rinv", u)][:],
-                in1=keepq[:, mg * T : (mg + NB) * T],
+                in1=keep[:, mg : mg + NB, :].rearrange("p m t -> p (m t)"),
                 op=ALU.mult,
             )
             for n in range(NB):
                 st[("rkeep", u + n)] = rkeep[:, n * T : (n + 1) * T]
 
         def ve_query_mask():
-            nc.vector.tensor_single_scalar(out=keepq[:], in_=st["kq_ps"][:, 0:NM], scalar=0.0, op=ALU.not_equal)
+            nc.vector.tensor_single_scalar(
+                out=keepq[:],
+                in_=st["tiles_ps"][:, :, 0 : B * NB].rearrange("p t m -> p m t"),
+                scalar=0.0,
+                op=ALU.not_equal,
+            )
 
         def ve_max(u, i):
             if not ok(u):
@@ -300,9 +297,14 @@ def tile_localselfattention_kernel(tc, Q, K, V, mask, out):
                 in1=st[("rkeep", u)][:, t0:t1].unsqueeze(2).to_broadcast([P, t1 - t0, D]),
                 op=ALU.mult,
             )
-            nc.sync.dma_start(
-                out=of[u * BS + t0 * P : u * BS + t1 * P, :].rearrange("(t p) d -> p t d", p=P), in_=o_sb[:]
-            )
+            rows = of[u * BS + t0 * P : u * BS + t1 * P, :]
+            if u < DIRECT:
+                nc.sync.dma_start(
+                    out=rows.rearrange("(h p w) d -> p h (w d)", p=P, w=2),
+                    in_=o_sb[:].rearrange("p (h w) d -> p h (w d)", w=2),
+                )
+            else:
+                nc.sync.dma_start(out=rows.rearrange("(t p) d -> p t d", p=P), in_=o_sb[:])
 
         def direct_copy(u, x, engine_copy):
             if x == 0:
@@ -353,16 +355,29 @@ def tile_localselfattention_kernel(tc, Q, K, V, mask, out):
                 in_=st[("eT_ps", u, t0)][:].rearrange("p i w q -> p i q w"),
             )
 
-        pe_direct_transposes(0)
+        pe_direct_transposes(0, 1)
+        pairs_ps = ps_x.tile([P, T, P], BF16, name="pairs_ps", tag="aux")
+        for c in range(T):
+            h, w = divmod(c, 2)
+            nc.tensor.transpose(pairs_ps[:, c, :], mrow[:, 256 * h + w : 256 * (h + 1) : 2], ident_bf[:])
+        pe_direct_transposes(0, 0)
+        pairs_mask = pairs_ps[:, :, 0 : B * NB].rearrange("p c m -> p m c")
+        bcol = const.tile([P, B * NB, T], F32, name="bcol")
+        nc.vector.tensor_scalar(
+            out=bcol[:], in0=pairs_mask, scalar1=0.0, scalar2=NEG, op0=ALU.is_equal, op1=ALU.mult
+        )
         direct_copy(0, 0, nc.vector.tensor_copy)
+        nc.vector.tensor_single_scalar(out=keep_direct[:], in_=pairs_mask, scalar=0.0, op=ALU.not_equal)
         direct_copy(0, 1, nc.scalar.copy)
-        bt_1, bcol_1 = mask_tile(1)
-        nc.scalar.copy(out=bt_1, in_=bcol_1)
+        for mg in (1, 0):
+            bt_mg, bcol_mg = mask_tile(mg)
+            nc.scalar.copy(out=bt_mg, in_=bcol_mg)
         for s in range(-20, 4 * UNITS + 20):
             u, i = divmod(s, 4)
             pe_scores(u, i)
             if s == 1:
-                pe_direct_transposes(1)
+                for x in range(2):
+                    pe_direct_transposes(1, x)
             if s == 5:
                 pe_query_mask()
             if i == 0:

@@ -63,15 +63,15 @@ def tile_localselfattention_kernel(tc, Q, K, V, mask, out):
             k_raw = loads.tile([P, T, D], BF16, name="k_raw", tag="k_raw")
             in_runs = "(h x w) d -> x h (w d)"
             out_runs = "x (h w) d -> x h (w d)"
-            nc.sync.dma_start(
-                out=q_raw[:].rearrange(out_runs, w=2), in_=qf[rows, :].rearrange(in_runs, x=P, w=2)
-            )
             if u < DIRECT:
                 nc.sync.dma_start(
                     out=k_raw[:].rearrange(out_runs, w=2), in_=kf[rows, :].rearrange(in_runs, x=P, w=2)
                 )
             else:
                 nc.sync.dma_start(out=k_raw[:], in_=kf[rows, :].rearrange("(p t) d -> p t d", t=T))
+            nc.sync.dma_start(
+                out=q_raw[:].rearrange(out_runs, w=2), in_=qf[rows, :].rearrange(in_runs, x=P, w=2)
+            )
             raw[u] = (q_raw, k_raw)
 
         def load_v(u):
@@ -83,9 +83,9 @@ def tile_localselfattention_kernel(tc, Q, K, V, mask, out):
             )
             raw_v[u] = v_raw
 
-        mrow = const.tile([P, BS], BF16, name="mrow")
-        nc.vector.memset(mrow[:], 0.0)
-        nc.scalar.dma_start(out=mrow[0 : B * NB, :], in_=mask.rearrange("b (n k) -> (b n) k", k=BS))
+        mrow = const.tile([P, BS // 2], BF16, name="mrow")
+        nc.gpsimd.memset(mrow[:], 0.0)
+        nc.scalar.dma_start(out=mrow[0 : 2 * B * NB, :], in_=mask.rearrange("b (m k) -> (b m) k", k=BS // 2))
         for u in range(DIRECT + 1):
             load_qk(u)
         warm = const.tile([P, BS], BF16, name="warm")
@@ -104,17 +104,20 @@ def tile_localselfattention_kernel(tc, Q, K, V, mask, out):
         make_identity(nc, ident_f[:])
 
         bt = const.tile([P, NM, P], F32, name="bt")
-        keep_direct = const.tile([P, B * NB, T], F32, name="keep_direct")
-        keepq = const.tile([P, B * NB, T], F32, name="keepq")
+        keep_direct = const.tile([P, 2 * B * NB, 2], F32, name="keep_direct")
+        keepq = const.tile([P, 2 * B * NB, 2], F32, name="keepq")
+
+        def bias_columns(mg):
+            return bcol[:, 2 * mg : 2 * mg + 2, :].rearrange("p h w -> p (h w)")
 
         def mask_tile(mg):
-            return bt[:, mg * T : (mg + 1) * T, :], bcol[:, mg, :].unsqueeze(2).to_broadcast([P, T, P])
+            return bt[:, mg * T : (mg + 1) * T, :], bias_columns(mg).unsqueeze(2).to_broadcast([P, T, P])
 
 
         def pe_query_mask():
-            tiles_ps = ps_x.tile([P, T, P], BF16, name="tiles_ps", tag="aux")
-            for t in range(T):
-                nc.tensor.transpose(tiles_ps[:, t, :], mrow[:, t * P : (t + 1) * P], ident_bf[:])
+            tiles_ps = ps_x.tile([P, 2, P], BF16, name="tiles_ps", tag="aux")
+            for j in range(2):
+                nc.tensor.transpose(tiles_ps[:, j, :], mrow[:, j * P : (j + 1) * P], ident_bf[:])
             st["tiles_ps"] = tiles_ps
 
         def pe_direct_transposes(u, x):
@@ -147,7 +150,7 @@ def tile_localselfattention_kernel(tc, Q, K, V, mask, out):
                 w, h = divmod(t, 2)
                 c = 2 * h + w
                 if u == 0:
-                    bias = bcol[:, mg, c : c + 1].to_broadcast([P, P])
+                    bias = bias_columns(mg)[:, c : c + 1].to_broadcast([P, P])
                 else:
                     bias = bt[:, mg * T + c, :]
                 nc.tensor.matmul(
@@ -171,7 +174,10 @@ def tile_localselfattention_kernel(tc, Q, K, V, mask, out):
             if not ok(u):
                 return
             if u == LAST:
-                eT_ps = ps_s.tile([P, t1 - t0, 2, P], F32, name="eT_ps", tag="s_ps")
+                eT_ps = ps_s.tile([P, 2, 2, P], F32, name="eT_ps", tag="s_ps")
+                nc.tensor.matmul(
+                    out=eT_ps[:].rearrange("p i w q -> p (i w q)"), lhsT=warm[:, 0:P], rhs=warm[:], start=True, stop=True
+                )
             else:
                 eT_ps = ps_x.tile([P, t1 - t0, 2, P], F32, name="eT_ps", tag="aux")
             for i in range(t0, t1):
@@ -231,7 +237,7 @@ def tile_localselfattention_kernel(tc, Q, K, V, mask, out):
             nc.gpsimd.tensor_tensor(
                 out=rkeep[:],
                 in0=st[("rinv", u)][:],
-                in1=keep[:, mg : mg + NB, :].rearrange("p m t -> p (m t)"),
+                in1=keep[:, 2 * mg : 2 * (mg + NB), :].rearrange("p m t -> p (m t)"),
                 op=ALU.mult,
             )
             for n in range(NB):
@@ -240,7 +246,7 @@ def tile_localselfattention_kernel(tc, Q, K, V, mask, out):
         def ve_query_mask():
             nc.vector.tensor_single_scalar(
                 out=keepq[:],
-                in_=st["tiles_ps"][:, :, 0 : B * NB].rearrange("p t m -> p m t"),
+                in_=st["tiles_ps"][:, :, 0 : 2 * B * NB].rearrange("p j m -> p m j"),
                 scalar=0.0,
                 op=ALU.not_equal,
             )
@@ -306,6 +312,19 @@ def tile_localselfattention_kernel(tc, Q, K, V, mask, out):
             else:
                 nc.sync.dma_start(out=rows.rearrange("(t p) d -> p t d", p=P), in_=o_sb[:])
 
+        def se_out(u):
+            o_sb = outs.tile([P, T, D], F32, name="o_sb", tag="o_sb")
+            for t in range(T):
+                nc.scalar.activation(
+                    out=o_sb[:, t, :],
+                    in_=st[("pv_ps", u, 0)][:, t, :],
+                    func=ACT.Copy,
+                    scale=st[("rkeep", u)][:, t : t + 1],
+                )
+            nc.sync.dma_start(
+                out=of[u * BS : (u + 1) * BS, :].rearrange("(t p) d -> p t d", p=P), in_=o_sb[:]
+            )
+
         def direct_copy(u, x, engine_copy):
             if x == 0:
                 st[("qkT", u)] = work.tile([P, 2 * BS], BF16, name="qkT", tag="qkT")
@@ -352,17 +371,16 @@ def tile_localselfattention_kernel(tc, Q, K, V, mask, out):
                 out=st[("eg", u)][:, t0 * P * T : t1 * P * T]
                 .bitcast(F32)
                 .rearrange("p (i q w) -> p i q w", i=t1 - t0, w=2),
-                in_=st[("eT_ps", u, t0)][:].rearrange("p i w q -> p i q w"),
+                in_=st[("eT_ps", u, t0)][:, 0 : t1 - t0, :, :].rearrange("p i w q -> p i q w"),
             )
 
         pe_direct_transposes(0, 1)
-        pairs_ps = ps_x.tile([P, T, P], BF16, name="pairs_ps", tag="aux")
-        for c in range(T):
-            h, w = divmod(c, 2)
-            nc.tensor.transpose(pairs_ps[:, c, :], mrow[:, 256 * h + w : 256 * (h + 1) : 2], ident_bf[:])
+        pairs_ps = ps_x.tile([P, 2, P], BF16, name="pairs_ps", tag="aux")
+        for w in range(2):
+            nc.tensor.transpose(pairs_ps[:, w, :], mrow[:, w::2], ident_bf[:])
         pe_direct_transposes(0, 0)
-        pairs_mask = pairs_ps[:, :, 0 : B * NB].rearrange("p c m -> p m c")
-        bcol = const.tile([P, B * NB, T], F32, name="bcol")
+        pairs_mask = pairs_ps[:, :, 0 : 2 * B * NB].rearrange("p w m -> p m w")
+        bcol = const.tile([P, 2 * B * NB, 2], F32, name="bcol")
         nc.vector.tensor_scalar(
             out=bcol[:], in0=pairs_mask, scalar1=0.0, scalar2=NEG, op0=ALU.is_equal, op1=ALU.mult
         )
@@ -417,7 +435,7 @@ def tile_localselfattention_kernel(tc, Q, K, V, mask, out):
                     for v in range(LAST - 2, UNITS):
                         ve_v_quantise(v)
             elif i == 2:
-                if u - 4 != LAST:
+                if u - 4 < LAST - 1:
                     ve_out(u - 4)
             tl = s - 10 - 4 * LAST
             if 0 <= tl < T:
@@ -456,3 +474,5 @@ def tile_localselfattention_kernel(tc, Q, K, V, mask, out):
             tl = s - 8 - 4 * LAST
             if 0 <= tl < T:
                 se_e_copy(LAST, tl, tl + 1)
+            if s == 4 * LAST + 15:
+                se_out(LAST - 1)

@@ -20,7 +20,6 @@ T = BS // P
 NM = B * NB * T
 LOAD_BUFS = 8
 V_BUFS = 5
-DIRECT = 2
 NEG = -10000.0
 NWARM = 5
 LAST = UNITS - 1
@@ -63,12 +62,9 @@ def tile_localselfattention_kernel(tc, Q, K, V, mask, out):
             k_raw = loads.tile([P, T, D], BF16, name="k_raw", tag="k_raw")
             in_runs = "(h x w) d -> x h (w d)"
             out_runs = "x (h w) d -> x h (w d)"
-            if u < DIRECT:
-                nc.sync.dma_start(
-                    out=k_raw[:].rearrange(out_runs, w=2), in_=kf[rows, :].rearrange(in_runs, x=P, w=2)
-                )
-            else:
-                nc.sync.dma_start(out=k_raw[:], in_=kf[rows, :].rearrange("(p t) d -> p t d", t=T))
+            nc.sync.dma_start(
+                out=k_raw[:].rearrange(out_runs, w=2), in_=kf[rows, :].rearrange(in_runs, x=P, w=2)
+            )
             nc.sync.dma_start(
                 out=q_raw[:].rearrange(out_runs, w=2), in_=qf[rows, :].rearrange(in_runs, x=P, w=2)
             )
@@ -86,7 +82,7 @@ def tile_localselfattention_kernel(tc, Q, K, V, mask, out):
         mrow = const.tile([P, BS // 2], BF16, name="mrow")
         nc.gpsimd.memset(mrow[:], 0.0)
         nc.scalar.dma_start(out=mrow[0 : 2 * B * NB, :], in_=mask.rearrange("b (m k) -> (b m) k", k=BS // 2))
-        for u in range(DIRECT + 1):
+        for u in range(3):
             load_qk(u)
         warm = const.tile([P, BS], BF16, name="warm")
         nc.vector.memset(warm[:], 0.0)
@@ -95,8 +91,8 @@ def tile_localselfattention_kernel(tc, Q, K, V, mask, out):
             nc.tensor.matmul(out=w_ps[:], lhsT=warm[:, 0:P], rhs=warm[:], start=True, stop=True)
         for u in range(LOAD_BUFS):
             load_v(u)
-            if DIRECT + 1 + u < LOAD_BUFS:
-                load_qk(DIRECT + 1 + u)
+            if 3 + u < LOAD_BUFS:
+                load_qk(3 + u)
 
         ident_bf = const.tile([P, P], BF16, name="ident_bf")
         make_identity(nc, ident_bf[:])
@@ -104,7 +100,6 @@ def tile_localselfattention_kernel(tc, Q, K, V, mask, out):
         make_identity(nc, ident_f[:])
 
         bt = const.tile([P, NM, P], F32, name="bt")
-        keep_direct = const.tile([P, 2 * B * NB, 2], F32, name="keep_direct")
         keepq = const.tile([P, 2 * B * NB, 2], F32, name="keepq")
 
         def bias_columns(mg):
@@ -114,31 +109,20 @@ def tile_localselfattention_kernel(tc, Q, K, V, mask, out):
             return bt[:, mg * T : (mg + 1) * T, :], bias_columns(mg).unsqueeze(2).to_broadcast([P, T, P])
 
 
-        def pe_query_mask():
-            tiles_ps = ps_x.tile([P, 2, P], BF16, name="tiles_ps", tag="aux")
-            for j in range(2):
-                nc.tensor.transpose(tiles_ps[:, j, :], mrow[:, j * P : (j + 1) * P], ident_bf[:])
-            st["tiles_ps"] = tiles_ps
-
-        def pe_direct_transposes(u, x):
-            order = ((0, 1, 2, 3), (0, 2, 1, 3))[x]
-            xT_ps = ps_x.tile([P, T, P], BF16, name="xT_ps", tag="aux")
-            for c in range(T):
-                nc.tensor.transpose(xT_ps[:, c, :], raw[u][x][:, order[c], :], ident_bf[:])
-            st[("xT_ps", u, x)] = xT_ps
-
-        def pe_qk_transposes(u):
-            if not DIRECT <= u < UNITS:
+        def pe_qk_transposes(u, parts):
+            if not ok(u):
                 return
-            qki = st[("qki", u)]
-            qkT_ps = ps_x.tile([P, T, P], F32, name="qkT_ps", tag="aux")
-            for c in range(T):
-                nc.tensor.transpose(
-                    qkT_ps[:, c, :],
-                    qki[:, c, :, :].rearrange("p d e -> p (d e)").bitcast(F32),
-                    ident_f[:],
-                )
-            st[("qkT_ps", u)] = qkT_ps
+            if u > 0:
+                qkT_ps = ps_x.tile([P, 2, T, P], BF16, name="qkT_ps", tag="aux")
+            for part in parts:
+                if u == 0:
+                    qkT_ps = ps_x.tile([P, 1, T, P], BF16, name="qkT_ps", tag="aux")
+                order = ((0, 1, 2, 3), (0, 2, 1, 3))[part]
+                for c in range(T):
+                    nc.tensor.transpose(
+                        qkT_ps[:, part if u > 0 else 0, c, :], raw[u][part][:, order[c], :], ident_bf[:]
+                    )
+                st[("qkT_ps", u, part)] = qkT_ps
 
         def pe_scores(u, i):
             if not ok(u):
@@ -220,36 +204,19 @@ def tile_localselfattention_kernel(tc, Q, K, V, mask, out):
                 raw_v[u][:].rearrange("p (e w) d -> p d w e", w=2),
             )
 
-        def gp_qk_pairs(u):
-            if not DIRECT <= u < UNITS:
-                return
-            qki = work.tile([P, T, D, 2], BF16, name="qki", tag="qki")
-            gp_copy(qki[:, 0:2, :, :], raw[u][0][:].rearrange("p (j e) d -> p j d e", e=2))
-            gp_copy(qki[:, 2:4, :, :], raw[u][1][:].rearrange("p (e w) d -> p w d e", w=2))
-            st[("qki", u)] = qki
-
         def gp_keep(u):
             if not ok(u):
                 return
             mg = mask_group(u)
-            keep = keep_direct if u < DIRECT else keepq
             rkeep = stat.tile([P, NB * T], F32, name="rkeep", tag="rkeep")
             nc.gpsimd.tensor_tensor(
                 out=rkeep[:],
                 in0=st[("rinv", u)][:],
-                in1=keep[:, 2 * mg : 2 * (mg + NB), :].rearrange("p m t -> p (m t)"),
+                in1=keepq[:, 2 * mg : 2 * (mg + NB), :].rearrange("p m t -> p (m t)"),
                 op=ALU.mult,
             )
             for n in range(NB):
                 st[("rkeep", u + n)] = rkeep[:, n * T : (n + 1) * T]
-
-        def ve_query_mask():
-            nc.vector.tensor_single_scalar(
-                out=keepq[:],
-                in_=st["tiles_ps"][:, :, 0 : 2 * B * NB].rearrange("p j m -> p m j"),
-                scalar=0.0,
-                op=ALU.not_equal,
-            )
 
         def ve_max(u, i):
             if not ok(u):
@@ -304,13 +271,10 @@ def tile_localselfattention_kernel(tc, Q, K, V, mask, out):
                 op=ALU.mult,
             )
             rows = of[u * BS + t0 * P : u * BS + t1 * P, :]
-            if u < DIRECT:
-                nc.sync.dma_start(
-                    out=rows.rearrange("(h p w) d -> p h (w d)", p=P, w=2),
-                    in_=o_sb[:].rearrange("p (h w) d -> p h (w d)", w=2),
-                )
-            else:
-                nc.sync.dma_start(out=rows.rearrange("(t p) d -> p t d", p=P), in_=o_sb[:])
+            nc.sync.dma_start(
+                out=rows.rearrange("(h p w) d -> p h (w d)", p=P, w=2),
+                in_=o_sb[:].rearrange("p (h w) d -> p h (w d)", w=2),
+            )
 
         def se_out(u):
             o_sb = outs.tile([P, T, D], F32, name="o_sb", tag="o_sb")
@@ -322,26 +286,24 @@ def tile_localselfattention_kernel(tc, Q, K, V, mask, out):
                     scale=st[("rkeep", u)][:, t : t + 1],
                 )
             nc.sync.dma_start(
-                out=of[u * BS : (u + 1) * BS, :].rearrange("(t p) d -> p t d", p=P), in_=o_sb[:]
+                out=of[u * BS : (u + 1) * BS, :].rearrange("(h p w) d -> p h (w d)", p=P, w=2),
+                in_=o_sb[:].rearrange("p (h w) d -> p h (w d)", w=2),
             )
 
-        def direct_copy(u, x, engine_copy):
-            if x == 0:
-                st[("qkT", u)] = work.tile([P, 2 * BS], BF16, name="qkT", tag="qkT")
-            engine_copy(
-                out=st[("qkT", u)][:, x * BS : (x + 1) * BS],
-                in_=st[("xT_ps", u, x)][:].rearrange("p c x -> p (c x)"),
-            )
+        def first_qk_copy():
+            qkT = work.tile([P, 2 * BS], BF16, name="qkT", tag="qkT")
+            for part, engine_copy in ((0, nc.vector.tensor_copy), (1, nc.scalar.copy)):
+                engine_copy(
+                    out=qkT[:, part * BS : (part + 1) * BS],
+                    in_=st[("qkT_ps", 0, part)][:].rearrange("p a c x -> p (a c x)"),
+                )
+            st[("qkT", 0)] = qkT
 
-        def qk_copy(u, on_vector):
-            if not DIRECT <= u < UNITS or (u % 2 == 0) != on_vector:
+        def qk_copy(u, engine_copy):
+            if not 0 < u < UNITS:
                 return
             qkT = work.tile([P, 2 * BS], BF16, name="qkT", tag="qkT")
-            words = st[("qkT_ps", u)][:].rearrange("p c x -> p (c x)")
-            if on_vector:
-                nc.vector.tensor_copy(out=qkT[:].bitcast(F32), in_=words)
-            else:
-                nc.scalar.copy(out=qkT[:].bitcast(F32), in_=words)
+            engine_copy(out=qkT[:], in_=st[("qkT_ps", u, 0)][:].rearrange("p a c x -> p (a c x)"))
             st[("qkT", u)] = qkT
 
         def se_exp(u, i):
@@ -374,19 +336,18 @@ def tile_localselfattention_kernel(tc, Q, K, V, mask, out):
                 in_=st[("eT_ps", u, t0)][:, 0 : t1 - t0, :, :].rearrange("p i w q -> p i q w"),
             )
 
-        pe_direct_transposes(0, 1)
+        pe_qk_transposes(0, (1,))
         pairs_ps = ps_x.tile([P, 2, P], BF16, name="pairs_ps", tag="aux")
         for w in range(2):
             nc.tensor.transpose(pairs_ps[:, w, :], mrow[:, w::2], ident_bf[:])
-        pe_direct_transposes(0, 0)
+        pe_qk_transposes(0, (0,))
         pairs_mask = pairs_ps[:, :, 0 : 2 * B * NB].rearrange("p w m -> p m w")
         bcol = const.tile([P, 2 * B * NB, 2], F32, name="bcol")
         nc.vector.tensor_scalar(
             out=bcol[:], in0=pairs_mask, scalar1=0.0, scalar2=NEG, op0=ALU.is_equal, op1=ALU.mult
         )
-        direct_copy(0, 0, nc.vector.tensor_copy)
-        nc.vector.tensor_single_scalar(out=keep_direct[:], in_=pairs_mask, scalar=0.0, op=ALU.not_equal)
-        direct_copy(0, 1, nc.scalar.copy)
+        first_qk_copy()
+        nc.vector.tensor_single_scalar(out=keepq[:], in_=pairs_mask, scalar=0.0, op=ALU.not_equal)
         for mg in (1, 0):
             bt_mg, bcol_mg = mask_tile(mg)
             nc.scalar.copy(out=bt_mg, in_=bcol_mg)
@@ -394,10 +355,7 @@ def tile_localselfattention_kernel(tc, Q, K, V, mask, out):
             u, i = divmod(s, 4)
             pe_scores(u, i)
             if s == 1:
-                for x in range(2):
-                    pe_direct_transposes(1, x)
-            if s == 5:
-                pe_query_mask()
+                pe_qk_transposes(1, (0, 1))
             if i == 0:
                 if u - 4 != LAST:
                     pe_pv(u - 4)
@@ -405,7 +363,8 @@ def tile_localselfattention_kernel(tc, Q, K, V, mask, out):
                 if u - 2 != LAST:
                     pe_e_transposes(u - 2, 2, 4)
             elif i == 2:
-                pe_qk_transposes(u + 2)
+                if u + 2 > 1:
+                    pe_qk_transposes(u + 2, (0, 1))
             else:
                 if u - 1 != LAST:
                     pe_e_transposes(u - 1, 0, 2)
@@ -418,12 +377,10 @@ def tile_localselfattention_kernel(tc, Q, K, V, mask, out):
             um, im = divmod(s - 2, 4)
             ve_max(um, im)
             if s == 3:
-                for x in range(2):
-                    direct_copy(1, x, nc.vector.tensor_copy)
-            if s == 7:
-                ve_query_mask()
+                qk_copy(1, nc.vector.tensor_copy)
             if i == 0:
-                qk_copy(u + 1, True)
+                if u % 2 == 1:
+                    qk_copy(u + 1, nc.vector.tensor_copy)
             elif i == 1:
                 if u - 3 != LAST:
                     ve_e_quantise(u - 3)
@@ -444,15 +401,9 @@ def tile_localselfattention_kernel(tc, Q, K, V, mask, out):
                 for t0 in range(0, T, 2):
                     ve_out(LAST, t0, t0 + 2)
             if i == 1:
-                if u + 2 < V_BUFS:
-                    gp_qk_pairs(u + 4)
-                    gp_v_regroup(u + 2)
-                else:
-                    gp_v_regroup(u + 2)
+                gp_v_regroup(u + 2)
                 if u % NB == 1:
                     gp_keep(u - 3)
-                if u + 2 >= V_BUFS:
-                    gp_qk_pairs(u + 4)
                 if H - B * NB + 2 <= u < H:
                     bt_u, bcol_u = mask_tile(u - H + B * NB)
                     gp_copy(bt_u, bcol_u)
@@ -464,7 +415,8 @@ def tile_localselfattention_kernel(tc, Q, K, V, mask, out):
             ux, ix = divmod(s - 4, 4)
             se_exp(ux, ix)
             if i == 0:
-                qk_copy(u + 1, False)
+                if u % 2 == 0 and u > 0:
+                    qk_copy(u + 1, nc.scalar.copy)
             elif i == 1:
                 if u - 2 != LAST:
                     se_e_copy(u - 2, 0, 2)

@@ -299,6 +299,9 @@ def tile_localselfattention_kernel(tc, Q, K, V, mask, out):
                 )
             st[("qkT", 0)] = qkT
 
+        def qk_on_vector(u):
+            return u % 7 in (0, 2, 4)
+
         def qk_copy(u, engine_copy):
             if not 0 < u < UNITS:
                 return
@@ -379,7 +382,7 @@ def tile_localselfattention_kernel(tc, Q, K, V, mask, out):
             if s == 3:
                 qk_copy(1, nc.vector.tensor_copy)
             if i == 0:
-                if u % 2 == 1:
+                if qk_on_vector(u + 1):
                     qk_copy(u + 1, nc.vector.tensor_copy)
             elif i == 1:
                 if u - 3 != LAST:
@@ -415,7 +418,7 @@ def tile_localselfattention_kernel(tc, Q, K, V, mask, out):
             ux, ix = divmod(s - 4, 4)
             se_exp(ux, ix)
             if i == 0:
-                if u % 2 == 0 and u > 0:
+                if u > 0 and not qk_on_vector(u + 1):
                     qk_copy(u + 1, nc.scalar.copy)
             elif i == 1:
                 if u - 2 != LAST:

@@ -19,7 +19,6 @@ UNITS = B * H * NB
 T = BS // P
 NM = B * NB * T
 LOAD_BUFS = 8
-V_BUFS = 5
 NEG = -10000.0
 NWARM = 5
 LAST = UNITS - 1
@@ -37,7 +36,7 @@ def tile_localselfattention_kernel(tc, Q, K, V, mask, out):
         ctx.enter_context(tc.manual_schedule())
         const = ctx.enter_context(tc.tile_pool(name="const", bufs=1))
         loads = ctx.enter_context(tc.tile_pool(name="loads", bufs=LOAD_BUFS))
-        vpool = ctx.enter_context(tc.tile_pool(name="vpool", bufs=V_BUFS))
+        vpool = ctx.enter_context(tc.tile_pool(name="vpool", bufs=3))
         work = ctx.enter_context(tc.tile_pool(name="work", bufs=3))
         outs = ctx.enter_context(tc.tile_pool(name="outs", bufs=6))
         stat = ctx.enter_context(tc.tile_pool(name="stat", bufs=8))
@@ -80,7 +79,7 @@ def tile_localselfattention_kernel(tc, Q, K, V, mask, out):
             raw_v[u] = v_raw
 
         mrow = const.tile([P, BS // 2], BF16, name="mrow")
-        nc.gpsimd.memset(mrow[:], 0.0)
+        nc.vector.memset(mrow[:], 0.0)
         nc.scalar.dma_start(out=mrow[0 : 2 * B * NB, :], in_=mask.rearrange("b (m k) -> (b m) k", k=BS // 2))
         for u in range(3):
             load_qk(u)
@@ -97,7 +96,7 @@ def tile_localselfattention_kernel(tc, Q, K, V, mask, out):
         ident_bf = const.tile([P, P], BF16, name="ident_bf")
         make_identity(nc, ident_bf[:])
         ident_f = const.tile([P, P], F32, name="ident_f")
-        make_identity(nc, ident_f[:])
+        nc.vector.tensor_copy(out=ident_f[:], in_=ident_bf[:])
 
         bt = const.tile([P, NM, P], F32, name="bt")
         keepq = const.tile([P, 2 * B * NB, 2], F32, name="keepq")
@@ -178,15 +177,16 @@ def tile_localselfattention_kernel(tc, Q, K, V, mask, out):
             if not ok(u):
                 return
             ecodes, escales = st[("eq", u)]
-            vcodes, vscales = st[("vq", u)]
+            vcodes, vscales = st[("vq", u // NB)]
+            v_cols = slice(u % NB * D, (u % NB + 1) * D)
             pv_ps = ps_x.tile([P, t1 - t0, D], F32, name="pv_ps", tag="aux")
             for i in range(t0, t1):
                 nc.tensor.matmul_mx(
                     out=pv_ps[:, i - t0, :],
                     lhsT=ecodes[:, i * P : (i + 1) * P].bitcast(FP8X4),
                     lhsT_scale=escales[:, i * P : (i + 1) * P],
-                    rhs=vcodes[:].bitcast(FP8X4),
-                    rhs_scale=vscales[:],
+                    rhs=vcodes[:, v_cols].bitcast(FP8X4),
+                    rhs_scale=vscales[:, v_cols],
                     start=True,
                     stop=True,
                 )
@@ -198,9 +198,11 @@ def tile_localselfattention_kernel(tc, Q, K, V, mask, out):
         def gp_v_regroup(u):
             if not ok(u):
                 return
-            st[("vg", u)] = vpool.tile([P, D, T], BF16, name="vg", tag="vg", align_bytes=64)
+            pair, n = divmod(u, NB)
+            if n == 0:
+                st[("vg", pair)] = vpool.tile([P, NB, D, T], BF16, name="vg", tag="vg", align_bytes=64)
             gp_copy(
-                st[("vg", u)][:].rearrange("p d (w e) -> p d w e", e=2),
+                st[("vg", pair)][:, n, :, :].rearrange("p d (w e) -> p d w e", e=2),
                 raw_v[u][:].rearrange("p (e w) d -> p d w e", w=2),
             )
 
@@ -230,14 +232,14 @@ def tile_localselfattention_kernel(tc, Q, K, V, mask, out):
         def ve_v_quantise(u):
             if not ok(u):
                 return
-            vcodes = vpool.tile([P, D], U32, name="vcodes", tag="vcodes", align_bytes=64)
-            vscales = vpool.tile([P, D], U8, name="vscales", tag="vscales", align_bytes=64)
+            vcodes = vpool.tile([P, NB * D], U32, name="vcodes", tag="vcodes", align_bytes=64)
+            vscales = vpool.tile([P, NB * D], U8, name="vscales", tag="vscales", align_bytes=64)
             nc.vector.quantize_mx(
                 out=vcodes[:].bitcast(FP8X4),
                 scales=vscales[:],
-                in_=st[("vg", u)][:].rearrange("p d j -> p (d j)"),
+                in_=st[("vg", u // NB)][:].rearrange("p n d j -> p (n d j)"),
             )
-            st[("vq", u)] = (vcodes, vscales)
+            st[("vq", u // NB)] = (vcodes, vscales)
 
         def ve_e_quantise(u, t0=0, t1=T):
             if not ok(u):
@@ -300,7 +302,7 @@ def tile_localselfattention_kernel(tc, Q, K, V, mask, out):
             st[("qkT", 0)] = qkT
 
         def qk_on_vector(u):
-            return u % 7 in (0, 2, 4)
+            return u % 7 in (0, 3, 5)
 
         def qk_copy(u, engine_copy):
             if not 0 < u < UNITS:
@@ -382,18 +384,17 @@ def tile_localselfattention_kernel(tc, Q, K, V, mask, out):
             if s == 3:
                 qk_copy(1, nc.vector.tensor_copy)
             if i == 0:
-                if qk_on_vector(u + 1):
+                if u > 0 and qk_on_vector(u + 1):
                     qk_copy(u + 1, nc.vector.tensor_copy)
             elif i == 1:
                 if u - 3 != LAST:
                     ve_e_quantise(u - 3)
                 if u % NB == 1:
                     ve_recip(u - 3)
-                if u - 3 < LAST - 2:
-                    ve_v_quantise(u - 3)
-                elif u - 3 == LAST - 2:
-                    for v in range(LAST - 2, UNITS):
-                        ve_v_quantise(v)
+                    if u - 3 < LAST - 1:
+                        ve_v_quantise(u - 3)
+                elif u - 2 == LAST - 1:
+                    ve_v_quantise(LAST - 1)
             elif i == 2:
                 if u - 4 < LAST - 1:
                     ve_out(u - 4)

@@ -111,7 +111,9 @@ def tile_localselfattention_kernel(tc, Q, K, V, mask, out):
         def pe_qk_transposes(u, parts):
             if not ok(u):
                 return
-            if u > 0:
+            if u == 1:
+                qkT_ps = ps_s.tile([P, 2, T, P], BF16, name="qkT_ps", tag="s_ps")
+            elif u > 1:
                 qkT_ps = ps_x.tile([P, 2, T, P], BF16, name="qkT_ps", tag="aux")
             for part in parts:
                 if u == 0:
@@ -346,21 +348,21 @@ def tile_localselfattention_kernel(tc, Q, K, V, mask, out):
         for w in range(2):
             nc.tensor.transpose(pairs_ps[:, w, :], mrow[:, w::2], ident_bf[:])
         pe_qk_transposes(0, (0,))
+        pe_qk_transposes(1, (0, 1))
         pairs_mask = pairs_ps[:, :, 0 : 2 * B * NB].rearrange("p w m -> p m w")
         bcol = const.tile([P, 2 * B * NB, 2], F32, name="bcol")
         nc.vector.tensor_scalar(
             out=bcol[:], in0=pairs_mask, scalar1=0.0, scalar2=NEG, op0=ALU.is_equal, op1=ALU.mult
         )
         first_qk_copy()
+        qk_copy(1, nc.scalar.copy)
         nc.vector.tensor_single_scalar(out=keepq[:], in_=pairs_mask, scalar=0.0, op=ALU.not_equal)
         for mg in (1, 0):
             bt_mg, bcol_mg = mask_tile(mg)
-            nc.scalar.copy(out=bt_mg, in_=bcol_mg)
+            nc.gpsimd.tensor_scalar(out=bt_mg, in0=bcol_mg, scalar1=1.0, scalar2=0.0, op0=ALU.mult, op1=ALU.add)
         for s in range(-20, 4 * UNITS + 20):
             u, i = divmod(s, 4)
             pe_scores(u, i)
-            if s == 1:
-                pe_qk_transposes(1, (0, 1))
             if i == 0:
                 if u - 4 != LAST:
                     pe_pv(u - 4)
@@ -381,8 +383,6 @@ def tile_localselfattention_kernel(tc, Q, K, V, mask, out):
                     pe_pv(LAST, t0, t0 + 2)
             um, im = divmod(s - 2, 4)
             ve_max(um, im)
-            if s == 3:
-                qk_copy(1, nc.vector.tensor_copy)
             if i == 0:
                 if u > 0 and qk_on_vector(u + 1):
                     qk_copy(u + 1, nc.vector.tensor_copy)
@@ -414,12 +414,14 @@ def tile_localselfattention_kernel(tc, Q, K, V, mask, out):
                 if ok(u):
                     load_qk(u + LOAD_BUFS)
                     load_v(u + LOAD_BUFS)
-            if s == 4 * LAST + 7:
+            if s == 4 * LAST + 6:
                 se_e_copy(LAST - 1, 2, 4)
             ux, ix = divmod(s - 4, 4)
             se_exp(ux, ix)
+            if s == 5:
+                qk_copy(2, nc.scalar.copy)
             if i == 0:
-                if u > 0 and not qk_on_vector(u + 1):
+                if u > 1 and not qk_on_vector(u + 1):
                     qk_copy(u + 1, nc.scalar.copy)
             elif i == 1:
                 if u - 2 != LAST:

from contextlib import ExitStack

import concourse.mybir as mybir
from concourse.masks import make_identity

BF16 = mybir.dt.bfloat16
F32 = mybir.dt.float32
U32 = mybir.dt.uint32
U8 = mybir.dt.uint8
FP8X4 = mybir.dt.float8_e4m3fn_x4
ALU = mybir.AluOpType
ACT = mybir.ActivationFunctionType
AX = mybir.AxisListType

P = 128
B, H, S, D, BS = 2, 12, 1024, 128, 512
NB = S // BS
UNITS = B * H * NB
T = BS // P
NM = B * NB * T
LOAD_BUFS = 8
NEG = -10000.0
NWARM = 5
LAST = UNITS - 1
FLOPS = 2 * 2 * BS * BS * D * UNITS


def tile_localselfattention_kernel(tc, Q, K, V, mask, out):
    nc = tc.nc
    qf = Q.flatten_outer_dims()
    kf = K.flatten_outer_dims()
    vf = V.flatten_outer_dims()
    of = out.flatten_outer_dims()

    with ExitStack() as ctx:
        ctx.enter_context(tc.manual_schedule())
        const = ctx.enter_context(tc.tile_pool(name="const", bufs=1))
        loads = ctx.enter_context(tc.tile_pool(name="loads", bufs=LOAD_BUFS))
        vpool = ctx.enter_context(tc.tile_pool(name="vpool", bufs=3))
        work = ctx.enter_context(tc.tile_pool(name="work", bufs=3))
        outs = ctx.enter_context(tc.tile_pool(name="outs", bufs=6))
        stat = ctx.enter_context(tc.tile_pool(name="stat", bufs=8))
        ps_s = ctx.enter_context(tc.psum_pool(name="ps_s", bufs=5))
        ps_x = ctx.enter_context(tc.psum_pool(name="ps_x", bufs=3))

        raw = {}
        raw_v = {}
        st = {}

        def ok(u):
            return 0 <= u < UNITS

        def mask_group(u):
            return (u // (H * NB)) * NB + u % NB

        def load_qk(u):
            if not ok(u):
                return
            rows = slice(u * BS, (u + 1) * BS)
            q_raw = loads.tile([P, T, D], BF16, name="q_raw", tag="q_raw")
            k_raw = loads.tile([P, T, D], BF16, name="k_raw", tag="k_raw")
            in_runs = "(h x w) d -> x h (w d)"
            out_runs = "x (h w) d -> x h (w d)"
            nc.sync.dma_start(
                out=k_raw[:].rearrange(out_runs, w=2), in_=kf[rows, :].rearrange(in_runs, x=P, w=2)
            )
            nc.sync.dma_start(
                out=q_raw[:].rearrange(out_runs, w=2), in_=qf[rows, :].rearrange(in_runs, x=P, w=2)
            )
            raw[u] = (q_raw, k_raw)

        def load_v(u):
            if not ok(u):
                return
            v_raw = loads.tile([P, T, D], BF16, name="v_raw", tag="v_raw")
            nc.sync.dma_start(
                out=v_raw[:], in_=vf[u * BS : (u + 1) * BS, :].rearrange("(p t) d -> p t d", t=T)
            )
            raw_v[u] = v_raw

        mrow = const.tile([P, BS // 2], BF16, name="mrow")
        nc.vector.memset(mrow[:], 0.0)
        nc.scalar.dma_start(out=mrow[0 : 2 * B * NB, :], in_=mask.rearrange("b (m k) -> (b m) k", k=BS // 2))
        for u in range(3):
            load_qk(u)
        warm = const.tile([P, BS], BF16, name="warm")
        nc.vector.memset(warm[:], 0.0)
        for k in range(NWARM):
            w_ps = ps_s.tile([P, BS], F32, name="w_ps", tag="s_ps")
            nc.tensor.matmul(out=w_ps[:], lhsT=warm[:, 0:P], rhs=warm[:], start=True, stop=True)
        for u in range(LOAD_BUFS):
            load_v(u)
            if 3 + u < LOAD_BUFS:
                load_qk(3 + u)

        ident_bf = const.tile([P, P], BF16, name="ident_bf")
        make_identity(nc, ident_bf[:])
        ident_f = const.tile([P, P], F32, name="ident_f")
        nc.vector.tensor_copy(out=ident_f[:], in_=ident_bf[:])

        bt = const.tile([P, NM, P], F32, name="bt")
        keepq = const.tile([P, 2 * B * NB, 2], F32, name="keepq")

        def bias_columns(mg):
            return bcol[:, 2 * mg : 2 * mg + 2, :].rearrange("p h w -> p (h w)")

        def mask_tile(mg):
            return bt[:, mg * T : (mg + 1) * T, :], bias_columns(mg).unsqueeze(2).to_broadcast([P, T, P])


        def pe_qk_transposes(u, parts):
            if not ok(u):
                return
            if u == 1:
                qkT_ps = ps_s.tile([P, 2, T, P], BF16, name="qkT_ps", tag="s_ps")
            elif u > 1:
                qkT_ps = ps_x.tile([P, 2, T, P], BF16, name="qkT_ps", tag="aux")
            for part in parts:
                if u == 0:
                    qkT_ps = ps_x.tile([P, 1, T, P], BF16, name="qkT_ps", tag="aux")
                order = ((0, 1, 2, 3), (0, 2, 1, 3))[part]
                for c in range(T):
                    nc.tensor.transpose(
                        qkT_ps[:, part if u > 0 else 0, c, :], raw[u][part][:, order[c], :], ident_bf[:]
                    )
                st[("qkT_ps", u, part)] = qkT_ps

        def pe_scores(u, i):
            if not ok(u):
                return
            mg = mask_group(u)
            qkT = st[("qkT", u)]
            s_ps = ps_s.tile([P, BS], F32, name="s_ps", tag="s_ps")
            for t in range(T):
                w, h = divmod(t, 2)
                c = 2 * h + w
                if u == 0:
                    bias = bias_columns(mg)[:, c : c + 1].to_broadcast([P, P])
                else:
                    bias = bt[:, mg * T + c, :]
                nc.tensor.matmul(
                    out=s_ps[:, t * P : (t + 1) * P],
                    lhsT=bias,
                    rhs=ident_f[:],
                    is_transpose=True,
                    start=(t == 0),
                    stop=False,
                )
            nc.tensor.matmul(
                out=s_ps[:],
                lhsT=qkT[:, i * P : (i + 1) * P],
                rhs=qkT[:, BS : 2 * BS],
                start=False,
                stop=True,
            )
            st[("s_ps", u, i)] = s_ps

        def pe_e_transposes(u, t0, t1):
            if not ok(u):
                return
            if u == LAST:
                eT_ps = ps_s.tile([P, 2, 2, P], F32, name="eT_ps", tag="s_ps")
                nc.tensor.matmul(
                    out=eT_ps[:].rearrange("p i w q -> p (i w q)"), lhsT=warm[:, 0:P], rhs=warm[:], start=True, stop=True
                )
            else:
                eT_ps = ps_x.tile([P, t1 - t0, 2, P], F32, name="eT_ps", tag="aux")
            for i in range(t0, t1):
                words = st[("e_sb", u, i // 2)][:, i % 2, :].bitcast(F32)
                for w in range(2):
                    nc.tensor.transpose(
                        eT_ps[:, i - t0, w, :],
                        words[:, w * P : (w + 1) * P],
                        ident_f[:],
                    )
            st[("eT_ps", u, t0)] = eT_ps

        def pe_pv(u, t0=0, t1=T):
            if not ok(u):
                return
            ecodes, escales = st[("eq", u)]
            vcodes, vscales = st[("vq", u // NB)]
            v_cols = slice(u % NB * D, (u % NB + 1) * D)
            pv_ps = ps_x.tile([P, t1 - t0, D], F32, name="pv_ps", tag="aux")
            for i in range(t0, t1):
                nc.tensor.matmul_mx(
                    out=pv_ps[:, i - t0, :],
                    lhsT=ecodes[:, i * P : (i + 1) * P].bitcast(FP8X4),
                    lhsT_scale=escales[:, i * P : (i + 1) * P],
                    rhs=vcodes[:, v_cols].bitcast(FP8X4),
                    rhs_scale=vscales[:, v_cols],
                    start=True,
                    stop=True,
                )
            st[("pv_ps", u, t0)] = pv_ps

        def gp_copy(out, in0):
            nc.gpsimd.tensor_scalar(out=out, in0=in0, scalar1=1.0, scalar2=0.0, op0=ALU.mult, op1=ALU.add)

        def gp_v_regroup(u):
            if not ok(u):
                return
            pair, n = divmod(u, NB)
            if n == 0:
                st[("vg", pair)] = vpool.tile([P, NB, D, T], BF16, name="vg", tag="vg", align_bytes=64)
            gp_copy(
                st[("vg", pair)][:, n, :, :].rearrange("p d (w e) -> p d w e", e=2),
                raw_v[u][:].rearrange("p (e w) d -> p d w e", w=2),
            )

        def gp_keep(u):
            if not ok(u):
                return
            mg = mask_group(u)
            rkeep = stat.tile([P, NB * T], F32, name="rkeep", tag="rkeep")
            nc.gpsimd.tensor_tensor(
                out=rkeep[:],
                in0=st[("rinv", u)][:],
                in1=keepq[:, 2 * mg : 2 * (mg + NB), :].rearrange("p m t -> p (m t)"),
                op=ALU.mult,
            )
            for n in range(NB):
                st[("rkeep", u + n)] = rkeep[:, n * T : (n + 1) * T]

        def ve_max(u, i):
            if not ok(u):
                return
            negm = stat.tile([P, 1], F32, name="negm", tag="negm")
            nc.vector.tensor_reduce(
                out=negm[:], in_=st[("s_ps", u, i)][:], axis=AX.X, op=ALU.max, negate=True
            )
            st[("negm", u, i)] = negm

        def ve_v_quantise(u):
            if not ok(u):
                return
            vcodes = vpool.tile([P, NB * D], U32, name="vcodes", tag="vcodes", align_bytes=64)
            vscales = vpool.tile([P, NB * D], U8, name="vscales", tag="vscales", align_bytes=64)
            nc.vector.quantize_mx(
                out=vcodes[:].bitcast(FP8X4),
                scales=vscales[:],
                in_=st[("vg", u // NB)][:].rearrange("p n d j -> p (n d j)"),
            )
            st[("vq", u // NB)] = (vcodes, vscales)

        def ve_e_quantise(u, t0=0, t1=T):
            if not ok(u):
                return
            if t0 == 0:
                ecodes = work.tile([P, BS], U32, name="ecodes", tag="ecodes", align_bytes=64)
                escales = work.tile([P, BS], U8, name="escales", tag="escales", align_bytes=64)
                st[("eq", u)] = (ecodes, escales)
            ecodes, escales = st[("eq", u)]
            nc.vector.quantize_mx(
                out=ecodes[:, t0 * P : t1 * P].bitcast(FP8X4),
                scales=escales[:, t0 * P : t1 * P],
                in_=st[("eg", u)][:, t0 * P * T : t1 * P * T],
            )

        def ve_recip(u):
            if not ok(u):
                return
            rinv = stat.tile([P, NB * T], F32, name="rinv", tag="rinv")
            nc.vector.reciprocal(out=rinv[:], in_=st[("rsum", u)][:])
            st[("rinv", u)] = rinv

        def ve_out(u, t0=0, t1=T):
            if not ok(u):
                return
            o_sb = outs.tile([P, t1 - t0, D], F32, name="o_sb", tag="o_sb")
            nc.vector.tensor_tensor(
                out=o_sb[:],
                in0=st[("pv_ps", u, t0)][:],
                in1=st[("rkeep", u)][:, t0:t1].unsqueeze(2).to_broadcast([P, t1 - t0, D]),
                op=ALU.mult,
            )
            rows = of[u * BS + t0 * P : u * BS + t1 * P, :]
            nc.sync.dma_start(
                out=rows.rearrange("(h p w) d -> p h (w d)", p=P, w=2),
                in_=o_sb[:].rearrange("p (h w) d -> p h (w d)", w=2),
            )

        def se_out(u):
            o_sb = outs.tile([P, T, D], F32, name="o_sb", tag="o_sb")
            for t in range(T):
                nc.scalar.activation(
                    out=o_sb[:, t, :],
                    in_=st[("pv_ps", u, 0)][:, t, :],
                    func=ACT.Copy,
                    scale=st[("rkeep", u)][:, t : t + 1],
                )
            nc.sync.dma_start(
                out=of[u * BS : (u + 1) * BS, :].rearrange("(h p w) d -> p h (w d)", p=P, w=2),
                in_=o_sb[:].rearrange("p (h w) d -> p h (w d)", w=2),
            )

        def first_qk_copy():
            qkT = work.tile([P, 2 * BS], BF16, name="qkT", tag="qkT")
            for part, engine_copy in ((0, nc.vector.tensor_copy), (1, nc.scalar.copy)):
                engine_copy(
                    out=qkT[:, part * BS : (part + 1) * BS],
                    in_=st[("qkT_ps", 0, part)][:].rearrange("p a c x -> p (a c x)"),
                )
            st[("qkT", 0)] = qkT

        def qk_on_vector(u):
            return u % 7 in (0, 3, 5)

        def qk_copy(u, engine_copy):
            if not 0 < u < UNITS:
                return
            qkT = work.tile([P, 2 * BS], BF16, name="qkT", tag="qkT")
            engine_copy(out=qkT[:], in_=st[("qkT_ps", u, 0)][:].rearrange("p a c x -> p (a c x)"))
            st[("qkT", u)] = qkT

        def se_exp(u, i):
            if not ok(u):
                return
            h, ii = divmod(i, 2)
            pair, n = divmod(u, NB)
            if n == 0 and i == 0:
                st[("rsum", u)] = stat.tile([P, NB * T], F32, name="rsum", tag="rsum")
            if ii == 0:
                st[("e_sb", u, h)] = work.tile([P, 2, BS], BF16, name="e_sb", tag="e_sb")
            nc.scalar.activation(
                out=st[("e_sb", u, h)][:, ii, :],
                in_=st[("s_ps", u, i)][:],
                func=ACT.Exp,
                bias=st[("negm", u, i)][:],
                scale=1.0,
                accum_out=st[("rsum", pair * NB)][:, n * T + i : n * T + i + 1],
            )

        def se_e_copy(u, t0, t1):
            if not ok(u):
                return
            if t0 == 0:
                st[("eg", u)] = work.tile([P, T * P * T], BF16, name="eg", tag="eg", align_bytes=64)
            nc.scalar.copy(
                out=st[("eg", u)][:, t0 * P * T : t1 * P * T]
                .bitcast(F32)
                .rearrange("p (i q w) -> p i q w", i=t1 - t0, w=2),
                in_=st[("eT_ps", u, t0)][:, 0 : t1 - t0, :, :].rearrange("p i w q -> p i q w"),
            )

        pe_qk_transposes(0, (1,))
        pairs_ps = ps_x.tile([P, 2, P], BF16, name="pairs_ps", tag="aux")
        for w in range(2):
            nc.tensor.transpose(pairs_ps[:, w, :], mrow[:, w::2], ident_bf[:])
        pe_qk_transposes(0, (0,))
        pe_qk_transposes(1, (0, 1))
        pairs_mask = pairs_ps[:, :, 0 : 2 * B * NB].rearrange("p w m -> p m w")
        bcol = const.tile([P, 2 * B * NB, 2], F32, name="bcol")
        nc.vector.tensor_scalar(
            out=bcol[:], in0=pairs_mask, scalar1=0.0, scalar2=NEG, op0=ALU.is_equal, op1=ALU.mult
        )
        first_qk_copy()
        qk_copy(1, nc.scalar.copy)
        nc.vector.tensor_single_scalar(out=keepq[:], in_=pairs_mask, scalar=0.0, op=ALU.not_equal)
        for mg in (1, 0):
            bt_mg, bcol_mg = mask_tile(mg)
            nc.gpsimd.tensor_scalar(out=bt_mg, in0=bcol_mg, scalar1=1.0, scalar2=0.0, op0=ALU.mult, op1=ALU.add)
        for s in range(-20, 4 * UNITS + 20):
            u, i = divmod(s, 4)
            pe_scores(u, i)
            if i == 0:
                if u - 4 != LAST:
                    pe_pv(u - 4)
            elif i == 1:
                if u - 2 != LAST:
                    pe_e_transposes(u - 2, 2, 4)
            elif i == 2:
                if u + 2 > 1:
                    pe_qk_transposes(u + 2, (0, 1))
            else:
                if u - 1 != LAST:
                    pe_e_transposes(u - 1, 0, 2)
            tl = s - 6 - 4 * LAST
            if 0 <= tl < T:
                pe_e_transposes(LAST, tl, tl + 1)
            if s == 4 * LAST + 15:
                for t0 in range(0, T, 2):
                    pe_pv(LAST, t0, t0 + 2)
            um, im = divmod(s - 2, 4)
            ve_max(um, im)
            if i == 0:
                if u > 0 and qk_on_vector(u + 1):
                    qk_copy(u + 1, nc.vector.tensor_copy)
            elif i == 1:
                if u - 3 != LAST:
                    ve_e_quantise(u - 3)
                if u % NB == 1:
                    ve_recip(u - 3)
                    if u - 3 < LAST - 1:
                        ve_v_quantise(u - 3)
                elif u - 2 == LAST - 1:
                    ve_v_quantise(LAST - 1)
            elif i == 2:
                if u - 4 < LAST - 1:
                    ve_out(u - 4)
            tl = s - 10 - 4 * LAST
            if 0 <= tl < T:
                ve_e_quantise(LAST, tl, tl + 1)
            if s == 4 * LAST + 17:
                for t0 in range(0, T, 2):
                    ve_out(LAST, t0, t0 + 2)
            if i == 1:
                gp_v_regroup(u + 2)
                if u % NB == 1:
                    gp_keep(u - 3)
                if H - B * NB + 2 <= u < H:
                    bt_u, bcol_u = mask_tile(u - H + B * NB)
                    gp_copy(bt_u, bcol_u)
                if ok(u):
                    load_qk(u + LOAD_BUFS)
                    load_v(u + LOAD_BUFS)
            if s == 4 * LAST + 6:
                se_e_copy(LAST - 1, 2, 4)
            ux, ix = divmod(s - 4, 4)
            se_exp(ux, ix)
            if s == 5:
                qk_copy(2, nc.scalar.copy)
            if i == 0:
                if u > 1 and not qk_on_vector(u + 1):
                    qk_copy(u + 1, nc.scalar.copy)
            elif i == 1:
                if u - 2 != LAST:
                    se_e_copy(u - 2, 0, 2)
            elif i == 3:
                if u - 2 < LAST - 1:
                    se_e_copy(u - 2, 2, 4)
            tl = s - 8 - 4 * LAST
            if 0 <= tl < T:
                se_e_copy(LAST, tl, tl + 1)
            if s == 4 * LAST + 15:
                se_out(LAST - 1)
